import numpy as np
import ml_dtypes


def mxq(x, axis, fmt="e4m3"):
    dtype, down = {"e4m3": (ml_dtypes.float8_e4m3fn, 7), "e5m2": (ml_dtypes.float8_e5m2, 14)}[fmt]
    v = np.moveaxis(np.asarray(x, np.float32).astype(ml_dtypes.bfloat16).astype(np.float64), axis, -1)
    blocks = v.reshape(v.shape[:-1] + (-1, 32))
    amax = np.abs(blocks).max(-1, keepdims=True)
    byte = np.maximum(np.where(amax > 0, np.frexp(amax)[1] - 1 + 127, 0) - down, 1)
    scale = np.exp2(byte - 127.0)
    codes = (blocks / scale).astype(np.float32).astype(dtype).astype(np.float64)
    return np.moveaxis((codes * scale).reshape(v.shape), -1, axis)


WIDE = False


def mx_kscale(k):
    if not WIDE:
        return np.ones(k)
    levels = np.array([10, -10, 5, -5, 0])
    a = np.random.permutation(np.resize(levels, k // 512 * 4)).reshape(k // 512, 4)
    idx = np.arange(k)
    return np.exp2(a[idx // 512, idx % 128 // 32])


BF16 = ml_dtypes.bfloat16


def bf(x):
    return np.asarray(x, np.float32).astype(BF16)


def f64(x):
    return np.asarray(x).astype(np.float64)


L, B, P, H, DH, DM = 2, 2, 129, 8, 64, 512
M = L + 1
K = L * H * DH
R = P - 1
THR = 0.001


def sg(v):
    return v


def setup_inputs():
    s = mx_kscale(K).reshape(L, H, DH)
    return {
        "attn_cache": bf(np.random.standard_normal((L, B, P, H, DH)) * s[:, None, None]),
        "mlp_cache": bf(np.random.standard_normal((M, B, P, DM)) / np.sqrt(M)),
        "mlp_mask": bf(np.random.uniform(0.0, 1.0, (B, M))),
        "attn_mask": bf(np.random.uniform(0.0, 1.0, (B, L, H))),
        "modal_attention": bf(np.random.standard_normal((L, H, DH)) * s),
        "modal_mlp": bf(np.random.standard_normal((M, DM)) / np.sqrt(M)),
        "W_O": bf(np.random.standard_normal((L, H, DH, DM)) * 2.0 / np.sqrt(K) / s[..., None]),
        "post_bias": bf(np.random.standard_normal((L, DM)) * 0.3 / np.sqrt(L)),
        "orig_in": bf(np.random.standard_normal((B, P, DM))),
    }


def reference(attn_cache, mlp_cache, mlp_mask, attn_mask, modal_attention, modal_mlp, W_O, post_bias, orig_in):
    modal_attention = f64(modal_attention)
    modal_mlp = f64(modal_mlp)
    mm = f64(mlp_mask)[:, None, :, None]
    mlp_stack = np.moveaxis(f64(mlp_cache), 0, 2)
    out = (mm * mlp_stack).sum(axis=2)
    mlp_blend = np.where(mm < THR, (1.0 - mm) * modal_mlp, (1.0 - mm) * sg(modal_mlp))
    out = out + mlp_blend.sum(axis=2)
    am = f64(attn_mask)[:, None, :, :, None]
    attn_stack = np.moveaxis(f64(attn_cache), 0, 2)
    attn_blend = np.where(am < THR, (1.0 - am) * modal_attention, (1.0 - am) * sg(modal_attention))
    attn_term = am * attn_stack + attn_blend
    attn_term = attn_term[:, 1:].reshape(B, R, K)
    attn_term = mxq(attn_term, 2, "e4m3") @ mxq(f64(W_O).reshape(K, DM), 0, "e4m3")
    out = out[:, 1:] + attn_term + f64(post_bias).sum(axis=0)
    return np.concatenate([sg(f64(orig_in)[:, :1]), out], axis=1)

@@ -1,0 +1,182 @@
+from contextlib import ExitStack
+
+import concourse.mybir as mybir
+from concourse.masks import make_identity
+
+BF16 = mybir.dt.bfloat16
+F32 = mybir.dt.float32
+U32 = mybir.dt.uint32
+U8 = mybir.dt.uint8
+FP8X4 = mybir.dt.float8_e4m3fn_x4
+ALU = mybir.AluOpType
+AX = mybir.AxisListType
+
+LAYERS, BATCH, POSITIONS, HEADS, D_HEAD, D_MODEL = 2, 2, 129, 8, 64, 512
+N_MLP = LAYERS + 1
+P = 128
+PACK = 4
+K_PASS = P * PACK
+N_CHUNKS = D_MODEL // P
+ROWS_PER_HEAD = D_HEAD // PACK
+
+FLOPS = 2 * BATCH * P * LAYERS * K_PASS * D_MODEL
+BYTES = (
+    2 * (LAYERS * BATCH * P * K_PASS + N_MLP * BATCH * P * D_MODEL + LAYERS * K_PASS * D_MODEL)
+    + 2 * (BATCH * N_MLP + BATCH * LAYERS * HEADS + LAYERS * K_PASS + (N_MLP + LAYERS + BATCH) * D_MODEL)
+    + 4 * BATCH * POSITIONS * D_MODEL
+)
+
+
+def tile_edgepruner_s_kernel(
+    tc, attn_cache, mlp_cache, mlp_mask, attn_mask, modal_attention, modal_mlp, W_O, post_bias, orig_in, out
+):
+    nc = tc.nc
+    with ExitStack() as ctx:
+        keep = ctx.enter_context(tc.tile_pool(name="keep", bufs=1))
+        psum = ctx.enter_context(tc.psum_pool(name="psum", bufs=1))
+
+        ident = keep.tile([P, P], F32)
+        make_identity(nc, ident[:])
+        small_rows = keep.tile([P, D_MODEL], BF16)
+        nc.vector.memset(small_rows[:], 0.0)
+        minus_one = keep.tile([P, BATCH], BF16)
+        nc.vector.memset(minus_one[:], 0.0)
+        nc.vector.memset(minus_one[0 : N_MLP + LAYERS, :], -1.0)
+        mask_rows = keep.tile([P, BATCH], BF16)
+        nc.vector.memset(mask_rows[:], 0.0)
+
+        x = keep.tile([P, BATCH, LAYERS, K_PASS], BF16)
+        for b in range(BATCH):
+            nc.sync.dma_start(out=x[:, b], in_=attn_cache[:, b, 1:POSITIONS].rearrange("l p h d -> p l (h d)"))
+        w = keep.tile([P, LAYERS, PACK, D_MODEL], BF16)
+        w_dram = W_O.rearrange("l h d n -> l (h d) n")
+        caches = keep.tile([P, BATCH, N_MLP, D_MODEL], BF16)
+        for i in range(LAYERS):
+            nc.sync.dma_start(out=w[:, i], in_=w_dram[i].rearrange("(p j) n -> p j n", j=PACK))
+            nc.sync.dma_start(out=caches[:, i], in_=mlp_cache[:, i, 1:POSITIONS].rearrange("m p n -> p m n"))
+
+        am_all = keep.tile([P, BATCH * LAYERS * HEADS], BF16)
+        nc.scalar.dma_start(out=am_all[:], in_=attn_mask.rearrange("b l h -> (b l h)").partition_broadcast(P))
+        modal = keep.tile([P, LAYERS, PACK], BF16)
+        nc.scalar.dma_start(
+            out=modal[:], in_=modal_attention.rearrange("l h d -> l (h d)").rearrange("l (p t) -> p l t", t=PACK)
+        )
+        nc.scalar.dma_start(out=small_rows[0:N_MLP, :], in_=modal_mlp)
+        nc.scalar.dma_start(out=small_rows[N_MLP : N_MLP + LAYERS, :], in_=post_bias)
+        with nc.allow_non_contiguous_dma(reason="six mask values, one row for each m"):
+            nc.scalar.dma_start(out=mask_rows[0:N_MLP, :], in_=mlp_mask.rearrange("b m -> m b"))
+        mm_bf = keep.tile([P, BATCH * N_MLP], BF16)
+        nc.scalar.dma_start(out=mm_bf[:], in_=mlp_mask.rearrange("b m -> (b m)").partition_broadcast(P))
+
+        first_bf = keep.tile([BATCH, D_MODEL], BF16)
+        nc.gpsimd.dma_start(out=first_bf[:], in_=orig_in[:, 0, :])
+        first = keep.tile([BATCH, D_MODEL], F32)
+        nc.gpsimd.tensor_copy(out=first[:], in_=first_bf[:])
+        nc.gpsimd.dma_start(out=out[:, 0, :], in_=first[:])
+
+        head_of_row = keep.tile([P, HEADS], F32)
+        nc.vector.tensor_reduce(
+            out=head_of_row[:], in_=ident[:].rearrange("p (h j) -> p h j", j=ROWS_PER_HEAD), axis=AX.X, op=ALU.add
+        )
+        am_picked = keep.tile([P, BATCH * LAYERS, HEADS], F32)
+        nc.vector.tensor_tensor(
+            out=am_picked[:],
+            in0=am_all[:].rearrange("p (c h) -> p c h", h=HEADS),
+            in1=head_of_row[:].unsqueeze(1).to_broadcast([P, BATCH * LAYERS, HEADS]),
+            op=ALU.mult,
+        )
+        am = keep.tile([P, BATCH, LAYERS], F32)
+        nc.vector.tensor_reduce(out=am[:].rearrange("p b l -> p (b l)"), in_=am_picked[:], axis=AX.X, op=ALU.add)
+        one_minus_am = keep.tile([P, BATCH, LAYERS], F32)
+        nc.vector.tensor_scalar(
+            out=one_minus_am[:], in0=am[:], scalar1=-1.0, scalar2=1.0, op0=ALU.mult, op1=ALU.add
+        )
+        modal_term = keep.tile([P, BATCH, LAYERS, PACK], F32)
+        nc.vector.tensor_tensor(
+            out=modal_term[:],
+            in0=modal[:].unsqueeze(1).to_broadcast([P, BATCH, LAYERS, PACK]),
+            in1=one_minus_am[:].unsqueeze(3).to_broadcast([P, BATCH, LAYERS, PACK]),
+            op=ALU.mult,
+        )
+        mm = keep.tile([P, BATCH, N_MLP], F32)
+        nc.vector.tensor_copy(out=mm[:].rearrange("p b m -> p (b m)"), in_=mm_bf[:])
+
+        neg_const = psum.tile([P, N_CHUNKS, BATCH], F32)
+        for c in range(N_CHUNKS):
+            chunk = small_rows[:, c * P : (c + 1) * P]
+            nc.tensor.matmul(out=neg_const[:, c, :], lhsT=chunk, rhs=minus_one[:], start=True, stop=False)
+            nc.tensor.matmul(out=neg_const[:, c, :], lhsT=chunk, rhs=mask_rows[:], start=False, stop=True)
+        const_col = keep.tile([P, N_CHUNKS, BATCH], F32)
+        nc.scalar.mul(const_col[:], neg_const[:], -1.0)
+
+        a_bf = keep.tile([P, BATCH, LAYERS, P, PACK], BF16, align_bytes=64)
+        a_codes = keep.tile([P, BATCH, LAYERS, P], U32, align_bytes=64)
+        a_scales = keep.tile([P, BATCH, LAYERS, P], U8, align_bytes=64)
+        for b in range(BATCH):
+            for l in range(LAYERS):
+                words = x[:, b, l, :].bitcast(F32).rearrange("p (w u) -> p u w", u=2)
+                x_t = psum.tile([P, P, 2], F32, tag="x_t", bufs=3, name="x_t%d%d" % (b, l))
+                for u in range(2):
+                    nc.tensor.transpose(x_t[:, :, u], words[:, u, :], ident[:])
+                nc.vector.scalar_tensor_tensor(
+                    out=a_bf[:, b, l],
+                    in0=x_t[:].rearrange("p r u -> p (r u)").bitcast(BF16).rearrange("p (r t) -> p r t", t=PACK),
+                    scalar=am[:, b, l : l + 1],
+                    in1=modal_term[:, b, l, :].unsqueeze(1).to_broadcast([P, P, PACK]),
+                    op0=ALU.mult,
+                    op1=ALU.add,
+                )
+            nc.vector.quantize_mx(
+                out=a_codes[:, b].rearrange("p l r -> p (l r)").bitcast(FP8X4),
+                scales=a_scales[:, b].rearrange("p l r -> p (l r)"),
+                in_=a_bf[:, b].rearrange("p l r t -> p (l r t)"),
+            )
+
+        const_all = []
+        for b in range(BATCH):
+            const_b = psum.tile([P, D_MODEL], F32, name="const_all%d" % b)
+            for c in range(N_CHUNKS):
+                nc.tensor.transpose(
+                    const_b[:, c * P : (c + 1) * P], const_col[:, c, b : b + 1].to_broadcast([P, P]), ident[:]
+                )
+            const_all.append(const_b)
+
+        w_grouped = keep.tile([P, LAYERS, D_MODEL, PACK], BF16, align_bytes=64)
+        w_codes = keep.tile([P, LAYERS, D_MODEL], U32, align_bytes=64)
+        w_scales = keep.tile([P, LAYERS, D_MODEL], U8, align_bytes=64)
+        for l in range(LAYERS):
+            nc.scalar.copy(
+                out=w_grouped[:, l].rearrange("p (g i) j -> p g j i", i=4),
+                in_=w[:, l].rearrange("p j (g i) -> p g j i", i=4),
+            )
+            nc.vector.quantize_mx(
+                out=w_codes[:, l].bitcast(FP8X4),
+                scales=w_scales[:, l],
+                in_=w_grouped[:, l].rearrange("p n j -> p (n j)"),
+            )
+
+        attn = [psum.tile([P, D_MODEL], F32, name="attn%d" % b) for b in range(BATCH)]
+        for l in range(LAYERS):
+            for b in range(BATCH):
+                nc.tensor.matmul_mx(
+                    out=attn[b][:],
+                    lhsT=a_codes[:, b, l].bitcast(FP8X4),
+                    lhsT_scale=a_scales[:, b, l],
+                    rhs=w_codes[:, l].bitcast(FP8X4),
+                    rhs_scale=w_scales[:, l],
+                    start=(l == 0),
+                    stop=(l == LAYERS - 1),
+                )
+
+        for b in range(BATCH):
+            mlp = keep.tile([P, D_MODEL], F32, name="mlp%d" % b)
+            nc.vector.scalar_tensor_tensor(
+                out=mlp[:], in0=caches[:, b, 0, :], scalar=mm[:, b, 0:1], in1=const_all[b][:], op0=ALU.mult, op1=ALU.add
+            )
+            for m in range(1, N_MLP):
+                nc.vector.scalar_tensor_tensor(
+                    out=mlp[:], in0=caches[:, b, m, :], scalar=mm[:, b, m : m + 1], in1=mlp[:], op0=ALU.mult, op1=ALU.add
+                )
+            result = keep.tile([P, D_MODEL], F32, name="result%d" % b)
+            nc.vector.tensor_tensor(out=result[:], in0=attn[b][:], in1=mlp[:], op=ALU.add)
+            nc.sync.dma_start(out=out[b, 1:POSITIONS, :], in_=result[:])

@@ -34,6 +34,7 @@ def tile_edgepruner_s_kernel(
     with ExitStack() as ctx:
         keep = ctx.enter_context(tc.tile_pool(name="keep", bufs=1))
         psum = ctx.enter_context(tc.psum_pool(name="psum", bufs=1))
+        ctx.enter_context(tc.manual_schedule())
 
         ident = keep.tile([P, P], F32)
         make_identity(nc, ident[:])
@@ -45,29 +46,28 @@ def tile_edgepruner_s_kernel(
         mask_rows = keep.tile([P, BATCH], BF16)
         nc.vector.memset(mask_rows[:], 0.0)
 
+        am_all = keep.tile([P, BATCH * LAYERS * HEADS], BF16)
+        nc.sync.dma_start(out=am_all[:], in_=attn_mask.rearrange("b l h -> (b l h)").partition_broadcast(P))
+        modal = keep.tile([P, LAYERS, PACK], BF16)
+        nc.sync.dma_start(
+            out=modal[:], in_=modal_attention.rearrange("l h d -> l (h d)").rearrange("l (p t) -> p l t", t=PACK)
+        )
         x = keep.tile([P, BATCH, LAYERS, K_PASS], BF16)
         for b in range(BATCH):
             nc.sync.dma_start(out=x[:, b], in_=attn_cache[:, b, 1:POSITIONS].rearrange("l p h d -> p l (h d)"))
+        nc.scalar.dma_start(out=small_rows[0:N_MLP, :], in_=modal_mlp)
+        nc.scalar.dma_start(out=small_rows[N_MLP : N_MLP + LAYERS, :], in_=post_bias)
+        mm_bf = keep.tile([P, BATCH * N_MLP], BF16)
+        nc.scalar.dma_start(out=mm_bf[:], in_=mlp_mask.rearrange("b m -> (b m)").partition_broadcast(P))
         w = keep.tile([P, LAYERS, PACK, D_MODEL], BF16)
         w_dram = W_O.rearrange("l h d n -> l (h d) n")
         caches = keep.tile([P, BATCH, N_MLP, D_MODEL], BF16)
-        for i in range(LAYERS):
-            nc.sync.dma_start(out=w[:, i], in_=w_dram[i].rearrange("(p j) n -> p j n", j=PACK))
-            nc.sync.dma_start(out=caches[:, i], in_=mlp_cache[:, i, 1:POSITIONS].rearrange("m p n -> p m n"))
-
-        am_all = keep.tile([P, BATCH * LAYERS * HEADS], BF16)
-        nc.scalar.dma_start(out=am_all[:], in_=attn_mask.rearrange("b l h -> (b l h)").partition_broadcast(P))
-        modal = keep.tile([P, LAYERS, PACK], BF16)
-        nc.scalar.dma_start(
-            out=modal[:], in_=modal_attention.rearrange("l h d -> l (h d)").rearrange("l (p t) -> p l t", t=PACK)
-        )
-        nc.scalar.dma_start(out=small_rows[0:N_MLP, :], in_=modal_mlp)
-        nc.scalar.dma_start(out=small_rows[N_MLP : N_MLP + LAYERS, :], in_=post_bias)
+        nc.sync.dma_start(out=w[:, 0], in_=w_dram[0].rearrange("(p j) n -> p j n", j=PACK))
+        nc.sync.dma_start(out=caches[:, 0], in_=mlp_cache[:, 0, 1:POSITIONS].rearrange("m p n -> p m n"))
+        nc.sync.dma_start(out=w[:, 1], in_=w_dram[1].rearrange("(p j) n -> p j n", j=PACK))
+        nc.sync.dma_start(out=caches[:, 1], in_=mlp_cache[:, 1, 1:POSITIONS].rearrange("m p n -> p m n"))
         with nc.allow_non_contiguous_dma(reason="six mask values, one row for each m"):
-            nc.scalar.dma_start(out=mask_rows[0:N_MLP, :], in_=mlp_mask.rearrange("b m -> m b"))
-        mm_bf = keep.tile([P, BATCH * N_MLP], BF16)
-        nc.scalar.dma_start(out=mm_bf[:], in_=mlp_mask.rearrange("b m -> (b m)").partition_broadcast(P))
-
+            nc.gpsimd.dma_start(out=mask_rows[0:N_MLP, :], in_=mlp_mask.rearrange("b m -> m b"))
         first_bf = keep.tile([BATCH, D_MODEL], BF16)
         nc.gpsimd.dma_start(out=first_bf[:], in_=orig_in[:, 0, :])
         first = keep.tile([BATCH, D_MODEL], F32)
@@ -98,48 +98,62 @@ def tile_edgepruner_s_kernel(
             in1=one_minus_am[:].unsqueeze(3).to_broadcast([P, BATCH, LAYERS, PACK]),
             op=ALU.mult,
         )
-        mm = keep.tile([P, BATCH, N_MLP], F32)
-        nc.vector.tensor_copy(out=mm[:].rearrange("p b m -> p (b m)"), in_=mm_bf[:])
-
-        neg_const = psum.tile([P, N_CHUNKS, BATCH], F32)
-        for c in range(N_CHUNKS):
-            chunk = small_rows[:, c * P : (c + 1) * P]
-            nc.tensor.matmul(out=neg_const[:, c, :], lhsT=chunk, rhs=minus_one[:], start=True, stop=False)
-            nc.tensor.matmul(out=neg_const[:, c, :], lhsT=chunk, rhs=mask_rows[:], start=False, stop=True)
-        const_col = keep.tile([P, N_CHUNKS, BATCH], F32)
-        nc.scalar.mul(const_col[:], neg_const[:], -1.0)
 
         a_bf = keep.tile([P, BATCH, LAYERS, P, PACK], BF16, align_bytes=64)
         a_codes = keep.tile([P, BATCH, LAYERS, P], U32, align_bytes=64)
         a_scales = keep.tile([P, BATCH, LAYERS, P], U8, align_bytes=64)
-        for b in range(BATCH):
-            for l in range(LAYERS):
-                words = x[:, b, l, :].bitcast(F32).rearrange("p (w u) -> p u w", u=2)
-                x_t = psum.tile([P, P, 2], F32, tag="x_t", bufs=3, name="x_t%d%d" % (b, l))
-                for u in range(2):
-                    nc.tensor.transpose(x_t[:, :, u], words[:, u, :], ident[:])
-                nc.vector.scalar_tensor_tensor(
-                    out=a_bf[:, b, l],
-                    in0=x_t[:].rearrange("p r u -> p (r u)").bitcast(BF16).rearrange("p (r t) -> p r t", t=PACK),
-                    scalar=am[:, b, l : l + 1],
-                    in1=modal_term[:, b, l, :].unsqueeze(1).to_broadcast([P, P, PACK]),
-                    op0=ALU.mult,
-                    op1=ALU.add,
-                )
+
+        def transpose_x(b, l):
+            words = x[:, b, l, :].bitcast(F32).rearrange("p (w u) -> p u w", u=2)
+            x_t = psum.tile([P, P, 2], F32, tag="x_t", bufs=3, name="x_t%d%d" % (b, l))
+            for u in range(2):
+                nc.tensor.transpose(x_t[:, :, u], words[:, u, :], ident[:])
+            return x_t
+
+        def blend(b, l, x_t):
+            nc.vector.scalar_tensor_tensor(
+                out=a_bf[:, b, l],
+                in0=x_t[:].rearrange("p r u -> p (r u)").bitcast(BF16).rearrange("p (r t) -> p r t", t=PACK),
+                scalar=am[:, b, l : l + 1],
+                in1=modal_term[:, b, l, :].unsqueeze(1).to_broadcast([P, P, PACK]),
+                op0=ALU.mult,
+                op1=ALU.add,
+            )
+
+        def quantise_a(b):
             nc.vector.quantize_mx(
                 out=a_codes[:, b].rearrange("p l r -> p (l r)").bitcast(FP8X4),
                 scales=a_scales[:, b].rearrange("p l r -> p (l r)"),
                 in_=a_bf[:, b].rearrange("p l r t -> p (l r t)"),
             )
 
-        const_all = []
+        x_t00 = transpose_x(0, 0)
+        x_t01 = transpose_x(0, 1)
+        x_t10 = transpose_x(1, 0)
+
+        neg_const = psum.tile([P, N_CHUNKS, BATCH], F32)
+        for c in range(N_CHUNKS):
+            chunk = small_rows[:, c * P : (c + 1) * P]
+            nc.tensor.matmul(out=neg_const[:, c, :], lhsT=chunk, rhs=minus_one[:], start=True, stop=False)
+            nc.tensor.matmul(out=neg_const[:, c, :], lhsT=chunk, rhs=mask_rows[:], start=False, stop=True)
+        neg_const_col = keep.tile([P, N_CHUNKS, BATCH], F32)
+        nc.scalar.copy(out=neg_const_col[:], in_=neg_const[:])
+
+        blend(0, 0, x_t00)
+        x_t11 = transpose_x(1, 1)
+        blend(0, 1, x_t01)
+        blend(1, 0, x_t10)
+        quantise_a(0)
+        blend(1, 1, x_t11)
+
+        neg_const_all = []
         for b in range(BATCH):
-            const_b = psum.tile([P, D_MODEL], F32, name="const_all%d" % b)
+            spread = psum.tile([P, D_MODEL], F32, name="neg_const_all%d" % b)
             for c in range(N_CHUNKS):
                 nc.tensor.transpose(
-                    const_b[:, c * P : (c + 1) * P], const_col[:, c, b : b + 1].to_broadcast([P, P]), ident[:]
+                    spread[:, c * P : (c + 1) * P], neg_const_col[:, c, b : b + 1].to_broadcast([P, P]), ident[:]
                 )
-            const_all.append(const_b)
+            neg_const_all.append(spread)
 
         w_grouped = keep.tile([P, LAYERS, D_MODEL, PACK], BF16, align_bytes=64)
         w_codes = keep.tile([P, LAYERS, D_MODEL], U32, align_bytes=64)
@@ -149,6 +163,8 @@ def tile_edgepruner_s_kernel(
                 out=w_grouped[:, l].rearrange("p (g i) j -> p g j i", i=4),
                 in_=w[:, l].rearrange("p j (g i) -> p g j i", i=4),
             )
+
+        def quantise_w(l):
             nc.vector.quantize_mx(
                 out=w_codes[:, l].bitcast(FP8X4),
                 scales=w_scales[:, l],
@@ -156,7 +172,8 @@ def tile_edgepruner_s_kernel(
             )
 
         attn = [psum.tile([P, D_MODEL], F32, name="attn%d" % b) for b in range(BATCH)]
-        for l in range(LAYERS):
+
+        def mx_passes(l):
             for b in range(BATCH):
                 nc.tensor.matmul_mx(
                     out=attn[b][:],
@@ -168,15 +185,32 @@ def tile_edgepruner_s_kernel(
                     stop=(l == LAYERS - 1),
                 )
 
-        for b in range(BATCH):
-            mlp = keep.tile([P, D_MODEL], F32, name="mlp%d" % b)
+        mm = keep.tile([P, BATCH, N_MLP], F32)
+        nc.vector.tensor_copy(out=mm[:].rearrange("p b m -> p (b m)"), in_=mm_bf[:])
+        mlp = [keep.tile([P, D_MODEL], F32, name="mlp%d" % b) for b in range(BATCH)]
+
+        def add_cache(b, m):
             nc.vector.scalar_tensor_tensor(
-                out=mlp[:], in0=caches[:, b, 0, :], scalar=mm[:, b, 0:1], in1=const_all[b][:], op0=ALU.mult, op1=ALU.add
+                out=mlp[b][:],
+                in0=caches[:, b, m, :],
+                scalar=mm[:, b, m : m + 1],
+                in1=(neg_const_all[b][:] if m == 0 else mlp[b][:]),
+                op0=ALU.mult,
+                op1=(ALU.subtract if m == 0 else ALU.add),
             )
-            for m in range(1, N_MLP):
-                nc.vector.scalar_tensor_tensor(
-                    out=mlp[:], in0=caches[:, b, m, :], scalar=mm[:, b, m : m + 1], in1=mlp[:], op0=ALU.mult, op1=ALU.add
-                )
+
+        add_cache(0, 0)
+        quantise_a(1)
+        add_cache(1, 0)
+        quantise_w(0)
+        mx_passes(0)
+        add_cache(0, 1)
+        add_cache(1, 1)
+        quantise_w(1)
+        mx_passes(1)
+        add_cache(0, 2)
+        add_cache(1, 2)
+        for b in range(BATCH):
             result = keep.tile([P, D_MODEL], F32, name="result%d" % b)
-            nc.vector.tensor_tensor(out=result[:], in0=attn[b][:], in1=mlp[:], op=ALU.add)
+            nc.vector.tensor_tensor(out=result[:], in0=attn[b][:], in1=mlp[b][:], op=ALU.add)
             nc.sync.dma_start(out=out[b, 1:POSITIONS, :], in_=result[:])

@@ -57,8 +57,8 @@ def tile_edgepruner_s_kernel(
             nc.sync.dma_start(out=x[:, b], in_=attn_cache[:, b, 1:POSITIONS].rearrange("l p h d -> p l (h d)"))
         nc.scalar.dma_start(out=small_rows[0:N_MLP, :], in_=modal_mlp)
         nc.scalar.dma_start(out=small_rows[N_MLP : N_MLP + LAYERS, :], in_=post_bias)
-        mm_bf = keep.tile([P, BATCH * N_MLP], BF16)
-        nc.scalar.dma_start(out=mm_bf[:], in_=mlp_mask.rearrange("b m -> (b m)").partition_broadcast(P))
+        with nc.allow_non_contiguous_dma(reason="six mask values, one row for each m"):
+            nc.scalar.dma_start(out=mask_rows[0:N_MLP, :], in_=mlp_mask.rearrange("b m -> m b"))
         w = keep.tile([P, LAYERS, PACK, D_MODEL], BF16)
         w_dram = W_O.rearrange("l h d n -> l (h d) n")
         caches = keep.tile([P, BATCH, N_MLP, D_MODEL], BF16)
@@ -66,8 +66,8 @@ def tile_edgepruner_s_kernel(
         nc.sync.dma_start(out=caches[:, 0], in_=mlp_cache[:, 0, 1:POSITIONS].rearrange("m p n -> p m n"))
         nc.sync.dma_start(out=w[:, 1], in_=w_dram[1].rearrange("(p j) n -> p j n", j=PACK))
         nc.sync.dma_start(out=caches[:, 1], in_=mlp_cache[:, 1, 1:POSITIONS].rearrange("m p n -> p m n"))
-        with nc.allow_non_contiguous_dma(reason="six mask values, one row for each m"):
-            nc.gpsimd.dma_start(out=mask_rows[0:N_MLP, :], in_=mlp_mask.rearrange("b m -> m b"))
+        mm_bf = keep.tile([P, BATCH * N_MLP], BF16)
+        nc.gpsimd.dma_start(out=mm_bf[:], in_=mlp_mask.rearrange("b m -> (b m)").partition_broadcast(P))
         first_bf = keep.tile([BATCH, D_MODEL], BF16)
         nc.gpsimd.dma_start(out=first_bf[:], in_=orig_in[:, 0, :])
         first = keep.tile([BATCH, D_MODEL], F32)
@@ -131,20 +131,21 @@ def tile_edgepruner_s_kernel(
         x_t01 = transpose_x(0, 1)
         x_t10 = transpose_x(1, 0)
 
+        blend(0, 0, x_t00)
+        x_t11 = transpose_x(1, 1)
+
         neg_const = psum.tile([P, N_CHUNKS, BATCH], F32)
         for c in range(N_CHUNKS):
             chunk = small_rows[:, c * P : (c + 1) * P]
             nc.tensor.matmul(out=neg_const[:, c, :], lhsT=chunk, rhs=minus_one[:], start=True, stop=False)
             nc.tensor.matmul(out=neg_const[:, c, :], lhsT=chunk, rhs=mask_rows[:], start=False, stop=True)
-        neg_const_col = keep.tile([P, N_CHUNKS, BATCH], F32)
-        nc.scalar.copy(out=neg_const_col[:], in_=neg_const[:])
 
-        blend(0, 0, x_t00)
-        x_t11 = transpose_x(1, 1)
         blend(0, 1, x_t01)
         blend(1, 0, x_t10)
         quantise_a(0)
         blend(1, 1, x_t11)
+        neg_const_col = keep.tile([P, N_CHUNKS, BATCH], F32)
+        nc.vector.tensor_copy(out=neg_const_col[:], in_=neg_const[:])
 
         neg_const_all = []
         for b in range(BATCH):
@@ -199,11 +200,11 @@ def tile_edgepruner_s_kernel(
                 op1=(ALU.subtract if m == 0 else ALU.add),
             )
 
-        add_cache(0, 0)
         quantise_a(1)
-        add_cache(1, 0)
         quantise_w(0)
         mx_passes(0)
+        add_cache(0, 0)
+        add_cache(1, 0)
         add_cache(0, 1)
         add_cache(1, 1)
         quantise_w(1)

@@ -38,6 +38,12 @@ def tile_edgepruner_s_kernel(
 
         ident = keep.tile([P, P], F32)
         make_identity(nc, ident[:])
+        am_rows = keep.tile([P, BATCH * LAYERS], BF16)
+        nc.vector.memset(am_rows[:], 0.0)
+        mm_row = keep.tile([P, BATCH * N_MLP], BF16)
+        nc.vector.memset(mm_row[:], 0.0)
+        ones = keep.tile([P, P], BF16)
+        nc.vector.memset(ones[:], 1.0)
         small_rows = keep.tile([P, D_MODEL], BF16)
         nc.vector.memset(small_rows[:], 0.0)
         minus_one = keep.tile([P, BATCH], BF16)
@@ -46,8 +52,8 @@ def tile_edgepruner_s_kernel(
         mask_rows = keep.tile([P, BATCH], BF16)
         nc.vector.memset(mask_rows[:], 0.0)
 
-        am_all = keep.tile([P, BATCH * LAYERS * HEADS], BF16)
-        nc.sync.dma_start(out=am_all[:], in_=attn_mask.rearrange("b l h -> (b l h)").partition_broadcast(P))
+        with nc.allow_non_contiguous_dma(reason="32 mask values, one row for each head"):
+            nc.sync.dma_start(out=am_rows[0:HEADS, :], in_=attn_mask.rearrange("b l h -> h (b l)"))
         modal = keep.tile([P, LAYERS, PACK], BF16)
         nc.sync.dma_start(
             out=modal[:], in_=modal_attention.rearrange("l h d -> l (h d)").rearrange("l (p t) -> p l t", t=PACK)
@@ -55,38 +61,34 @@ def tile_edgepruner_s_kernel(
         x = keep.tile([P, BATCH, LAYERS, K_PASS], BF16)
         for b in range(BATCH):
             nc.sync.dma_start(out=x[:, b], in_=attn_cache[:, b, 1:POSITIONS].rearrange("l p h d -> p l (h d)"))
+        w = keep.tile([P, LAYERS, PACK, D_MODEL], BF16)
+        w_dram = W_O.rearrange("l h d n -> l (h d) n")
+        nc.sync.dma_start(out=w[:, 0], in_=w_dram[0].rearrange("(p j) n -> p j n", j=PACK))
         nc.scalar.dma_start(out=small_rows[0:N_MLP, :], in_=modal_mlp)
         nc.scalar.dma_start(out=small_rows[N_MLP : N_MLP + LAYERS, :], in_=post_bias)
         with nc.allow_non_contiguous_dma(reason="six mask values, one row for each m"):
             nc.scalar.dma_start(out=mask_rows[0:N_MLP, :], in_=mlp_mask.rearrange("b m -> m b"))
-        w = keep.tile([P, LAYERS, PACK, D_MODEL], BF16)
-        w_dram = W_O.rearrange("l h d n -> l (h d) n")
+        nc.scalar.dma_start(out=mm_row[0:1, :], in_=mlp_mask.rearrange("b m -> (b m)").unsqueeze(0))
         caches = keep.tile([P, BATCH, N_MLP, D_MODEL], BF16)
-        nc.sync.dma_start(out=w[:, 0], in_=w_dram[0].rearrange("(p j) n -> p j n", j=PACK))
         nc.sync.dma_start(out=caches[:, 0], in_=mlp_cache[:, 0, 1:POSITIONS].rearrange("m p n -> p m n"))
         nc.sync.dma_start(out=w[:, 1], in_=w_dram[1].rearrange("(p j) n -> p j n", j=PACK))
         nc.sync.dma_start(out=caches[:, 1], in_=mlp_cache[:, 1, 1:POSITIONS].rearrange("m p n -> p m n"))
-        mm_bf = keep.tile([P, BATCH * N_MLP], BF16)
-        nc.gpsimd.dma_start(out=mm_bf[:], in_=mlp_mask.rearrange("b m -> (b m)").partition_broadcast(P))
         first_bf = keep.tile([BATCH, D_MODEL], BF16)
         nc.gpsimd.dma_start(out=first_bf[:], in_=orig_in[:, 0, :])
         first = keep.tile([BATCH, D_MODEL], F32)
         nc.gpsimd.tensor_copy(out=first[:], in_=first_bf[:])
         nc.gpsimd.dma_start(out=out[:, 0, :], in_=first[:])
 
-        head_of_row = keep.tile([P, HEADS], F32)
-        nc.vector.tensor_reduce(
-            out=head_of_row[:], in_=ident[:].rearrange("p (h j) -> p h j", j=ROWS_PER_HEAD), axis=AX.X, op=ALU.add
+        head_rows = keep.tile([P, HEADS, ROWS_PER_HEAD], BF16)
+        nc.vector.tensor_copy(
+            out=head_rows[:], in_=ident[:, 0:HEADS].unsqueeze(2).to_broadcast([P, HEADS, ROWS_PER_HEAD])
         )
-        am_picked = keep.tile([P, BATCH * LAYERS, HEADS], F32)
-        nc.vector.tensor_tensor(
-            out=am_picked[:],
-            in0=am_all[:].rearrange("p (c h) -> p c h", h=HEADS),
-            in1=head_of_row[:].unsqueeze(1).to_broadcast([P, BATCH * LAYERS, HEADS]),
-            op=ALU.mult,
+        am_spread = psum.tile([P, BATCH * LAYERS], F32, tag="x_t", bufs=3)
+        nc.tensor.matmul(
+            out=am_spread[:], lhsT=head_rows[:].rearrange("q h j -> q (h j)"), rhs=am_rows[:], start=True, stop=True
         )
         am = keep.tile([P, BATCH, LAYERS], F32)
-        nc.vector.tensor_reduce(out=am[:].rearrange("p b l -> p (b l)"), in_=am_picked[:], axis=AX.X, op=ALU.add)
+        nc.vector.tensor_copy(out=am[:].rearrange("p b l -> p (b l)"), in_=am_spread[:])
         one_minus_am = keep.tile([P, BATCH, LAYERS], F32)
         nc.vector.tensor_scalar(
             out=one_minus_am[:], in0=am[:], scalar1=-1.0, scalar2=1.0, op0=ALU.mult, op1=ALU.add
@@ -134,18 +136,22 @@ def tile_edgepruner_s_kernel(
         blend(0, 0, x_t00)
         x_t11 = transpose_x(1, 1)
 
-        neg_const = psum.tile([P, N_CHUNKS, BATCH], F32)
+        small_sums = psum.tile([P, N_CHUNKS * BATCH + BATCH * N_MLP], F32)
+        neg_const = small_sums[:, 0 : N_CHUNKS * BATCH].rearrange("p (c b) -> p c b", b=BATCH)
         for c in range(N_CHUNKS):
             chunk = small_rows[:, c * P : (c + 1) * P]
             nc.tensor.matmul(out=neg_const[:, c, :], lhsT=chunk, rhs=minus_one[:], start=True, stop=False)
             nc.tensor.matmul(out=neg_const[:, c, :], lhsT=chunk, rhs=mask_rows[:], start=False, stop=True)
+        nc.tensor.matmul(out=small_sums[:, N_CHUNKS * BATCH :], lhsT=ones[:], rhs=mm_row[:], start=True, stop=True)
 
         blend(0, 1, x_t01)
         blend(1, 0, x_t10)
         quantise_a(0)
         blend(1, 1, x_t11)
-        neg_const_col = keep.tile([P, N_CHUNKS, BATCH], F32)
-        nc.vector.tensor_copy(out=neg_const_col[:], in_=neg_const[:])
+        small_sb = keep.tile([P, N_CHUNKS * BATCH + BATCH * N_MLP], F32)
+        nc.vector.tensor_copy(out=small_sb[:], in_=small_sums[:])
+        neg_const_col = small_sb[:, 0 : N_CHUNKS * BATCH].rearrange("p (c b) -> p c b", b=BATCH)
+        mm = small_sb[:, N_CHUNKS * BATCH :].rearrange("p (b m) -> p b m", m=N_MLP)
 
         neg_const_all = []
         for b in range(BATCH):
@@ -186,8 +192,6 @@ def tile_edgepruner_s_kernel(
                     stop=(l == LAYERS - 1),
                 )
 
-        mm = keep.tile([P, BATCH, N_MLP], F32)
-        nc.vector.tensor_copy(out=mm[:].rearrange("p b m -> p (b m)"), in_=mm_bf[:])
         mlp = [keep.tile([P, D_MODEL], F32, name="mlp%d" % b) for b in range(BATCH)]
 
         def add_cache(b, m):

@@ -18,6 +18,8 @@ PACK = 4
 K_PASS = P * PACK
 N_CHUNKS = D_MODEL // P
 ROWS_PER_HEAD = D_HEAD // PACK
+N_AM = BATCH * LAYERS
+N_MM = BATCH * N_MLP
 
 FLOPS = 2 * BATCH * P * LAYERS * K_PASS * D_MODEL
 BYTES = (
@@ -36,14 +38,10 @@ def tile_edgepruner_s_kernel(
         psum = ctx.enter_context(tc.psum_pool(name="psum", bufs=1))
         ctx.enter_context(tc.manual_schedule())
 
+        masks_in = keep.tile([P, N_AM + N_MM], BF16)
+        nc.gpsimd.memset(masks_in[:], 0.0)
         ident = keep.tile([P, P], F32)
         make_identity(nc, ident[:])
-        am_rows = keep.tile([P, BATCH * LAYERS], BF16)
-        nc.vector.memset(am_rows[:], 0.0)
-        mm_row = keep.tile([P, BATCH * N_MLP], BF16)
-        nc.vector.memset(mm_row[:], 0.0)
-        ones = keep.tile([P, P], BF16)
-        nc.vector.memset(ones[:], 1.0)
         small_rows = keep.tile([P, D_MODEL], BF16)
         nc.vector.memset(small_rows[:], 0.0)
         minus_one = keep.tile([P, BATCH], BF16)
@@ -53,22 +51,22 @@ def tile_edgepruner_s_kernel(
         nc.vector.memset(mask_rows[:], 0.0)
 
         with nc.allow_non_contiguous_dma(reason="32 mask values, one row for each head"):
-            nc.sync.dma_start(out=am_rows[0:HEADS, :], in_=attn_mask.rearrange("b l h -> h (b l)"))
+            nc.sync.dma_start(out=masks_in[0:HEADS, 0:N_AM], in_=attn_mask.rearrange("b l h -> h (b l)"))
+        nc.sync.dma_start(out=masks_in[HEADS : HEADS + 1, N_AM:], in_=mlp_mask.rearrange("b m -> (b m)").unsqueeze(0))
         modal = keep.tile([P, LAYERS, PACK], BF16)
         nc.sync.dma_start(
             out=modal[:], in_=modal_attention.rearrange("l h d -> l (h d)").rearrange("l (p t) -> p l t", t=PACK)
         )
+        nc.scalar.dma_start(out=small_rows[0:N_MLP, :], in_=modal_mlp)
+        nc.scalar.dma_start(out=small_rows[N_MLP : N_MLP + LAYERS, :], in_=post_bias)
         x = keep.tile([P, BATCH, LAYERS, K_PASS], BF16)
         for b in range(BATCH):
             nc.sync.dma_start(out=x[:, b], in_=attn_cache[:, b, 1:POSITIONS].rearrange("l p h d -> p l (h d)"))
         w = keep.tile([P, LAYERS, PACK, D_MODEL], BF16)
         w_dram = W_O.rearrange("l h d n -> l (h d) n")
         nc.sync.dma_start(out=w[:, 0], in_=w_dram[0].rearrange("(p j) n -> p j n", j=PACK))
-        nc.scalar.dma_start(out=small_rows[0:N_MLP, :], in_=modal_mlp)
-        nc.scalar.dma_start(out=small_rows[N_MLP : N_MLP + LAYERS, :], in_=post_bias)
         with nc.allow_non_contiguous_dma(reason="six mask values, one row for each m"):
             nc.scalar.dma_start(out=mask_rows[0:N_MLP, :], in_=mlp_mask.rearrange("b m -> m b"))
-        nc.scalar.dma_start(out=mm_row[0:1, :], in_=mlp_mask.rearrange("b m -> (b m)").unsqueeze(0))
         caches = keep.tile([P, BATCH, N_MLP, D_MODEL], BF16)
         nc.sync.dma_start(out=caches[:, 0], in_=mlp_cache[:, 0, 1:POSITIONS].rearrange("m p n -> p m n"))
         nc.sync.dma_start(out=w[:, 1], in_=w_dram[1].rearrange("(p j) n -> p j n", j=PACK))
@@ -79,19 +77,24 @@ def tile_edgepruner_s_kernel(
         nc.gpsimd.tensor_copy(out=first[:], in_=first_bf[:])
         nc.gpsimd.dma_start(out=out[:, 0, :], in_=first[:])
 
-        head_rows = keep.tile([P, HEADS, ROWS_PER_HEAD], BF16)
-        nc.vector.tensor_copy(
-            out=head_rows[:], in_=ident[:, 0:HEADS].unsqueeze(2).to_broadcast([P, HEADS, ROWS_PER_HEAD])
+        spread = keep.tile([P, HEADS, ROWS_PER_HEAD], BF16)
+        nc.vector.tensor_tensor(
+            out=spread[:],
+            in0=ident[:, 0:HEADS].unsqueeze(2).to_broadcast([P, HEADS, ROWS_PER_HEAD]),
+            in1=ident[:, HEADS : HEADS + 1].unsqueeze(2).to_broadcast([P, HEADS, ROWS_PER_HEAD]),
+            op=ALU.add,
         )
-        am_spread = psum.tile([P, BATCH * LAYERS], F32, tag="x_t", bufs=3)
+        masks_ps = psum.tile([P, N_AM + N_MM], F32, tag="x_t", bufs=3)
         nc.tensor.matmul(
-            out=am_spread[:], lhsT=head_rows[:].rearrange("q h j -> q (h j)"), rhs=am_rows[:], start=True, stop=True
+            out=masks_ps[:], lhsT=spread[:].rearrange("q h j -> q (h j)"), rhs=masks_in[:], start=True, stop=True
         )
-        am = keep.tile([P, BATCH, LAYERS], F32)
-        nc.vector.tensor_copy(out=am[:].rearrange("p b l -> p (b l)"), in_=am_spread[:])
+        mask_values = keep.tile([P, N_AM + N_MM], F32)
+        nc.vector.tensor_copy(out=mask_values[:], in_=masks_ps[:])
+        am = mask_values[:, 0:N_AM].rearrange("p (b l) -> p b l", l=LAYERS)
+        mm = mask_values[:, N_AM:].rearrange("p (b m) -> p b m", m=N_MLP)
         one_minus_am = keep.tile([P, BATCH, LAYERS], F32)
         nc.vector.tensor_scalar(
-            out=one_minus_am[:], in0=am[:], scalar1=-1.0, scalar2=1.0, op0=ALU.mult, op1=ALU.add
+            out=one_minus_am[:], in0=am, scalar1=-1.0, scalar2=1.0, op0=ALU.mult, op1=ALU.add
         )
         modal_term = keep.tile([P, BATCH, LAYERS, PACK], F32)
         nc.vector.tensor_tensor(
@@ -136,31 +139,28 @@ def tile_edgepruner_s_kernel(
         blend(0, 0, x_t00)
         x_t11 = transpose_x(1, 1)
 
-        small_sums = psum.tile([P, N_CHUNKS * BATCH + BATCH * N_MLP], F32)
-        neg_const = small_sums[:, 0 : N_CHUNKS * BATCH].rearrange("p (c b) -> p c b", b=BATCH)
+        neg_const = psum.tile([P, N_CHUNKS, BATCH], F32)
         for c in range(N_CHUNKS):
             chunk = small_rows[:, c * P : (c + 1) * P]
             nc.tensor.matmul(out=neg_const[:, c, :], lhsT=chunk, rhs=minus_one[:], start=True, stop=False)
             nc.tensor.matmul(out=neg_const[:, c, :], lhsT=chunk, rhs=mask_rows[:], start=False, stop=True)
-        nc.tensor.matmul(out=small_sums[:, N_CHUNKS * BATCH :], lhsT=ones[:], rhs=mm_row[:], start=True, stop=True)
 
         blend(0, 1, x_t01)
         blend(1, 0, x_t10)
         quantise_a(0)
         blend(1, 1, x_t11)
-        small_sb = keep.tile([P, N_CHUNKS * BATCH + BATCH * N_MLP], F32)
-        nc.vector.tensor_copy(out=small_sb[:], in_=small_sums[:])
-        neg_const_col = small_sb[:, 0 : N_CHUNKS * BATCH].rearrange("p (c b) -> p c b", b=BATCH)
-        mm = small_sb[:, N_CHUNKS * BATCH :].rearrange("p (b m) -> p b m", m=N_MLP)
+        quantise_a(1)
+        neg_const_col = keep.tile([P, N_CHUNKS, BATCH], F32)
+        nc.vector.tensor_copy(out=neg_const_col[:], in_=neg_const[:])
 
         neg_const_all = []
         for b in range(BATCH):
-            spread = psum.tile([P, D_MODEL], F32, name="neg_const_all%d" % b)
+            repeated = psum.tile([P, D_MODEL], F32, name="neg_const_all%d" % b)
             for c in range(N_CHUNKS):
                 nc.tensor.transpose(
-                    spread[:, c * P : (c + 1) * P], neg_const_col[:, c, b : b + 1].to_broadcast([P, P]), ident[:]
+                    repeated[:, c * P : (c + 1) * P], neg_const_col[:, c, b : b + 1].to_broadcast([P, P]), ident[:]
                 )
-            neg_const_all.append(spread)
+            neg_const_all.append(repeated)
 
         w_grouped = keep.tile([P, LAYERS, D_MODEL, PACK], BF16, align_bytes=64)
         w_codes = keep.tile([P, LAYERS, D_MODEL], U32, align_bytes=64)
@@ -204,7 +204,6 @@ def tile_edgepruner_s_kernel(
                 op1=(ALU.subtract if m == 0 else ALU.add),
             )
 
-        quantise_a(1)
         quantise_w(0)
         mx_passes(0)
         add_cache(0, 0)

@@ -18,8 +18,6 @@ PACK = 4
 K_PASS = P * PACK
 N_CHUNKS = D_MODEL // P
 ROWS_PER_HEAD = D_HEAD // PACK
-N_AM = BATCH * LAYERS
-N_MM = BATCH * N_MLP
 
 FLOPS = 2 * BATCH * P * LAYERS * K_PASS * D_MODEL
 BYTES = (
@@ -38,10 +36,15 @@ def tile_edgepruner_s_kernel(
         psum = ctx.enter_context(tc.psum_pool(name="psum", bufs=1))
         ctx.enter_context(tc.manual_schedule())
 
-        masks_in = keep.tile([P, N_AM + N_MM], BF16)
-        nc.gpsimd.memset(masks_in[:], 0.0)
+        am_rows = keep.tile([P, BATCH * LAYERS], BF16)
+        nc.vector.memset(am_rows[:], 0.0)
         ident = keep.tile([P, P], F32)
-        make_identity(nc, ident[:])
+        nc.vector.memset(ident[:], 0.0)
+        make_identity(nc, ident[:], nomemset=True)
+        mm_row = keep.tile([P, BATCH * N_MLP], BF16)
+        nc.vector.memset(mm_row[:], 0.0)
+        ones = keep.tile([P, P], BF16)
+        nc.vector.memset(ones[:], 1.0)
         small_rows = keep.tile([P, D_MODEL], BF16)
         nc.vector.memset(small_rows[:], 0.0)
         minus_one = keep.tile([P, BATCH], BF16)
@@ -50,23 +53,23 @@ def tile_edgepruner_s_kernel(
         mask_rows = keep.tile([P, BATCH], BF16)
         nc.vector.memset(mask_rows[:], 0.0)
 
+        x = keep.tile([P, BATCH, LAYERS, K_PASS], BF16)
+        nc.sync.dma_start(out=x[:, 0], in_=attn_cache[:, 0, 1:POSITIONS].rearrange("l p h d -> p l (h d)"))
         with nc.allow_non_contiguous_dma(reason="32 mask values, one row for each head"):
-            nc.sync.dma_start(out=masks_in[0:HEADS, 0:N_AM], in_=attn_mask.rearrange("b l h -> h (b l)"))
-        nc.sync.dma_start(out=masks_in[HEADS : HEADS + 1, N_AM:], in_=mlp_mask.rearrange("b m -> (b m)").unsqueeze(0))
+            nc.sync.dma_start(out=am_rows[0:HEADS, :], in_=attn_mask.rearrange("b l h -> h (b l)"))
         modal = keep.tile([P, LAYERS, PACK], BF16)
         nc.sync.dma_start(
             out=modal[:], in_=modal_attention.rearrange("l h d -> l (h d)").rearrange("l (p t) -> p l t", t=PACK)
         )
-        nc.scalar.dma_start(out=small_rows[0:N_MLP, :], in_=modal_mlp)
-        nc.scalar.dma_start(out=small_rows[N_MLP : N_MLP + LAYERS, :], in_=post_bias)
-        x = keep.tile([P, BATCH, LAYERS, K_PASS], BF16)
-        for b in range(BATCH):
-            nc.sync.dma_start(out=x[:, b], in_=attn_cache[:, b, 1:POSITIONS].rearrange("l p h d -> p l (h d)"))
+        nc.sync.dma_start(out=x[:, 1], in_=attn_cache[:, 1, 1:POSITIONS].rearrange("l p h d -> p l (h d)"))
         w = keep.tile([P, LAYERS, PACK, D_MODEL], BF16)
         w_dram = W_O.rearrange("l h d n -> l (h d) n")
         nc.sync.dma_start(out=w[:, 0], in_=w_dram[0].rearrange("(p j) n -> p j n", j=PACK))
+        nc.scalar.dma_start(out=small_rows[0:N_MLP, :], in_=modal_mlp)
+        nc.scalar.dma_start(out=small_rows[N_MLP : N_MLP + LAYERS, :], in_=post_bias)
         with nc.allow_non_contiguous_dma(reason="six mask values, one row for each m"):
             nc.scalar.dma_start(out=mask_rows[0:N_MLP, :], in_=mlp_mask.rearrange("b m -> m b"))
+        nc.scalar.dma_start(out=mm_row[0:1, :], in_=mlp_mask.rearrange("b m -> (b m)").unsqueeze(0))
         caches = keep.tile([P, BATCH, N_MLP, D_MODEL], BF16)
         nc.sync.dma_start(out=caches[:, 0], in_=mlp_cache[:, 0, 1:POSITIONS].rearrange("m p n -> p m n"))
         nc.sync.dma_start(out=w[:, 1], in_=w_dram[1].rearrange("(p j) n -> p j n", j=PACK))
@@ -77,24 +80,19 @@ def tile_edgepruner_s_kernel(
         nc.gpsimd.tensor_copy(out=first[:], in_=first_bf[:])
         nc.gpsimd.dma_start(out=out[:, 0, :], in_=first[:])
 
-        spread = keep.tile([P, HEADS, ROWS_PER_HEAD], BF16)
-        nc.vector.tensor_tensor(
-            out=spread[:],
-            in0=ident[:, 0:HEADS].unsqueeze(2).to_broadcast([P, HEADS, ROWS_PER_HEAD]),
-            in1=ident[:, HEADS : HEADS + 1].unsqueeze(2).to_broadcast([P, HEADS, ROWS_PER_HEAD]),
-            op=ALU.add,
+        head_rows = keep.tile([P, HEADS, ROWS_PER_HEAD], BF16)
+        nc.vector.tensor_copy(
+            out=head_rows[:], in_=ident[:, 0:HEADS].unsqueeze(2).to_broadcast([P, HEADS, ROWS_PER_HEAD])
         )
-        masks_ps = psum.tile([P, N_AM + N_MM], F32, tag="x_t", bufs=3)
+        am_spread = psum.tile([P, BATCH * LAYERS], F32, tag="x_t", bufs=3)
         nc.tensor.matmul(
-            out=masks_ps[:], lhsT=spread[:].rearrange("q h j -> q (h j)"), rhs=masks_in[:], start=True, stop=True
+            out=am_spread[:], lhsT=head_rows[:].rearrange("q h j -> q (h j)"), rhs=am_rows[:], start=True, stop=True
         )
-        mask_values = keep.tile([P, N_AM + N_MM], F32)
-        nc.vector.tensor_copy(out=mask_values[:], in_=masks_ps[:])
-        am = mask_values[:, 0:N_AM].rearrange("p (b l) -> p b l", l=LAYERS)
-        mm = mask_values[:, N_AM:].rearrange("p (b m) -> p b m", m=N_MLP)
+        am = keep.tile([P, BATCH, LAYERS], F32)
+        nc.vector.tensor_copy(out=am[:].rearrange("p b l -> p (b l)"), in_=am_spread[:])
         one_minus_am = keep.tile([P, BATCH, LAYERS], F32)
         nc.vector.tensor_scalar(
-            out=one_minus_am[:], in0=am, scalar1=-1.0, scalar2=1.0, op0=ALU.mult, op1=ALU.add
+            out=one_minus_am[:], in0=am[:], scalar1=-1.0, scalar2=1.0, op0=ALU.mult, op1=ALU.add
         )
         modal_term = keep.tile([P, BATCH, LAYERS, PACK], F32)
         nc.vector.tensor_tensor(
@@ -139,28 +137,31 @@ def tile_edgepruner_s_kernel(
         blend(0, 0, x_t00)
         x_t11 = transpose_x(1, 1)
 
-        neg_const = psum.tile([P, N_CHUNKS, BATCH], F32)
+        small_sums = psum.tile([P, N_CHUNKS * BATCH + BATCH * N_MLP], F32)
+        neg_const = small_sums[:, 0 : N_CHUNKS * BATCH].rearrange("p (c b) -> p c b", b=BATCH)
         for c in range(N_CHUNKS):
             chunk = small_rows[:, c * P : (c + 1) * P]
             nc.tensor.matmul(out=neg_const[:, c, :], lhsT=chunk, rhs=minus_one[:], start=True, stop=False)
             nc.tensor.matmul(out=neg_const[:, c, :], lhsT=chunk, rhs=mask_rows[:], start=False, stop=True)
+        nc.tensor.matmul(out=small_sums[:, N_CHUNKS * BATCH :], lhsT=ones[:], rhs=mm_row[:], start=True, stop=True)
 
         blend(0, 1, x_t01)
         blend(1, 0, x_t10)
         quantise_a(0)
         blend(1, 1, x_t11)
-        quantise_a(1)
-        neg_const_col = keep.tile([P, N_CHUNKS, BATCH], F32)
-        nc.vector.tensor_copy(out=neg_const_col[:], in_=neg_const[:])
+        small_sb = keep.tile([P, N_CHUNKS * BATCH + BATCH * N_MLP], F32)
+        nc.vector.tensor_copy(out=small_sb[:], in_=small_sums[:])
+        neg_const_col = small_sb[:, 0 : N_CHUNKS * BATCH].rearrange("p (c b) -> p c b", b=BATCH)
+        mm = small_sb[:, N_CHUNKS * BATCH :].rearrange("p (b m) -> p b m", m=N_MLP)
 
         neg_const_all = []
         for b in range(BATCH):
-            repeated = psum.tile([P, D_MODEL], F32, name="neg_const_all%d" % b)
+            spread = psum.tile([P, D_MODEL], F32, name="neg_const_all%d" % b)
             for c in range(N_CHUNKS):
                 nc.tensor.transpose(
-                    repeated[:, c * P : (c + 1) * P], neg_const_col[:, c, b : b + 1].to_broadcast([P, P]), ident[:]
+                    spread[:, c * P : (c + 1) * P], neg_const_col[:, c, b : b + 1].to_broadcast([P, P]), ident[:]
                 )
-            neg_const_all.append(repeated)
+            neg_const_all.append(spread)
 
         w_grouped = keep.tile([P, LAYERS, D_MODEL, PACK], BF16, align_bytes=64)
         w_codes = keep.tile([P, LAYERS, D_MODEL], U32, align_bytes=64)
@@ -204,6 +205,7 @@ def tile_edgepruner_s_kernel(
                 op1=(ALU.subtract if m == 0 else ALU.add),
             )
 
+        quantise_a(1)
         quantise_w(0)
         mx_passes(0)
         add_cache(0, 0)

@@ -69,6 +69,8 @@ def tile_edgepruner_s_kernel(
         nc.scalar.dma_start(out=small_rows[N_MLP : N_MLP + LAYERS, :], in_=post_bias)
         with nc.allow_non_contiguous_dma(reason="six mask values, one row for each m"):
             nc.scalar.dma_start(out=mask_rows[0:N_MLP, :], in_=mlp_mask.rearrange("b m -> m b"))
+        table_warm = keep.tile([P, 1], BF16)
+        nc.scalar.copy(out=table_warm[:], in_=ones[:, 0:1])
         nc.scalar.dma_start(out=mm_row[0:1, :], in_=mlp_mask.rearrange("b m -> (b m)").unsqueeze(0))
         caches = keep.tile([P, BATCH, N_MLP, D_MODEL], BF16)
         nc.sync.dma_start(out=caches[:, 0], in_=mlp_cache[:, 0, 1:POSITIONS].rearrange("m p n -> p m n"))

@@ -72,10 +72,13 @@ def tile_edgepruner_s_kernel(
         table_warm = keep.tile([P, 1], BF16)
         nc.scalar.copy(out=table_warm[:], in_=ones[:, 0:1])
         nc.scalar.dma_start(out=mm_row[0:1, :], in_=mlp_mask.rearrange("b m -> (b m)").unsqueeze(0))
-        caches = keep.tile([P, BATCH, N_MLP, D_MODEL], BF16)
-        nc.sync.dma_start(out=caches[:, 0], in_=mlp_cache[:, 0, 1:POSITIONS].rearrange("m p n -> p m n"))
+        caches = keep.tile([P, N_MLP, BATCH, D_MODEL], BF16)
+        nc.sync.dma_start(
+            out=caches[:, 0:2].rearrange("p m b n -> p (m b) n"),
+            in_=mlp_cache[0:2, :, 1:POSITIONS].rearrange("m b p n -> p (m b) n"),
+        )
         nc.sync.dma_start(out=w[:, 1], in_=w_dram[1].rearrange("(p j) n -> p j n", j=PACK))
-        nc.sync.dma_start(out=caches[:, 1], in_=mlp_cache[:, 1, 1:POSITIONS].rearrange("m p n -> p m n"))
+        nc.sync.dma_start(out=caches[:, 2], in_=mlp_cache[2, :, 1:POSITIONS].rearrange("b p n -> p b n"))
         first_bf = keep.tile([BATCH, D_MODEL], BF16)
         nc.gpsimd.dma_start(out=first_bf[:], in_=orig_in[:, 0, :])
         first = keep.tile([BATCH, D_MODEL], F32)
@@ -200,7 +203,7 @@ def tile_edgepruner_s_kernel(
         def add_cache(b, m):
             nc.vector.scalar_tensor_tensor(
                 out=mlp[b][:],
-                in0=caches[:, b, m, :],
+                in0=caches[:, m, b, :],
                 scalar=mm[:, b, m : m + 1],
                 in1=(neg_const_all[b][:] if m == 0 else mlp[b][:]),
                 op0=ALU.mult,

@@ -80,10 +80,10 @@ def tile_edgepruner_s_kernel(
         nc.sync.dma_start(out=w[:, 1], in_=w_dram[1].rearrange("(p j) n -> p j n", j=PACK))
         nc.sync.dma_start(out=caches[:, 2], in_=mlp_cache[2, :, 1:POSITIONS].rearrange("b p n -> p b n"))
         first_bf = keep.tile([BATCH, D_MODEL], BF16)
-        nc.gpsimd.dma_start(out=first_bf[:], in_=orig_in[:, 0, :])
+        nc.sync.dma_start(out=first_bf[:], in_=orig_in[:, 0, :])
         first = keep.tile([BATCH, D_MODEL], F32)
         nc.gpsimd.tensor_copy(out=first[:], in_=first_bf[:])
-        nc.gpsimd.dma_start(out=out[:, 0, :], in_=first[:])
+        nc.sync.dma_start(out=out[:, 0, :], in_=first[:])
 
         head_rows = keep.tile([P, HEADS, ROWS_PER_HEAD], BF16)
         nc.vector.tensor_copy(

@@ -81,9 +81,6 @@ def tile_edgepruner_s_kernel(
         nc.sync.dma_start(out=caches[:, 2], in_=mlp_cache[2, :, 1:POSITIONS].rearrange("b p n -> p b n"))
         first_bf = keep.tile([BATCH, D_MODEL], BF16)
         nc.sync.dma_start(out=first_bf[:], in_=orig_in[:, 0, :])
-        first = keep.tile([BATCH, D_MODEL], F32)
-        nc.gpsimd.tensor_copy(out=first[:], in_=first_bf[:])
-        nc.sync.dma_start(out=out[:, 0, :], in_=first[:])
 
         head_rows = keep.tile([P, HEADS, ROWS_PER_HEAD], BF16)
         nc.vector.tensor_copy(
@@ -176,6 +173,10 @@ def tile_edgepruner_s_kernel(
                 out=w_grouped[:, l].rearrange("p (g i) j -> p g j i", i=4),
                 in_=w[:, l].rearrange("p j (g i) -> p g j i", i=4),
             )
+
+        first = keep.tile([BATCH, D_MODEL], F32)
+        nc.scalar.copy(out=first[:], in_=first_bf[:])
+        nc.sync.dma_start(out=out[:, 0, :], in_=first[:])
 
         def quantise_w(l):
             nc.vector.quantize_mx(

@@ -16,7 +16,9 @@ N_MLP = LAYERS + 1
 P = 128
 PACK = 4
 K_PASS = P * PACK
-N_CHUNKS = D_MODEL // P
+NI = D_MODEL // P
+FIRST_M = (1, 0)
+MM_COL = 16
 ROWS_PER_HEAD = D_HEAD // PACK
 
 FLOPS = 2 * BATCH * P * LAYERS * K_PASS * D_MODEL
@@ -36,27 +38,19 @@ def tile_edgepruner_s_kernel(
         psum = ctx.enter_context(tc.psum_pool(name="psum", bufs=1))
         ctx.enter_context(tc.manual_schedule())
 
-        am_rows = keep.tile([P, BATCH * LAYERS], BF16)
-        nc.vector.memset(am_rows[:], 0.0)
+        mask_rows = keep.tile([P, MM_COL + N_MLP], BF16)
+        nc.gpsimd.memset(mask_rows[:], 0.0)
         ident = keep.tile([P, P], F32)
         nc.vector.memset(ident[:], 0.0)
         make_identity(nc, ident[:], nomemset=True)
-        mm_row = keep.tile([P, BATCH * N_MLP], BF16)
-        nc.vector.memset(mm_row[:], 0.0)
-        ones = keep.tile([P, P], BF16)
-        nc.vector.memset(ones[:], 1.0)
-        small_rows = keep.tile([P, D_MODEL], BF16)
-        nc.vector.memset(small_rows[:], 0.0)
-        minus_one = keep.tile([P, BATCH], BF16)
-        nc.vector.memset(minus_one[:], 0.0)
-        nc.vector.memset(minus_one[0 : N_MLP + LAYERS, :], -1.0)
-        mask_rows = keep.tile([P, BATCH], BF16)
-        nc.vector.memset(mask_rows[:], 0.0)
+        warm_in = keep.tile([P, 1], BF16)
+        nc.vector.memset(warm_in[:], 0.0)
 
         x = keep.tile([P, BATCH, LAYERS, K_PASS], BF16)
         nc.sync.dma_start(out=x[:, 0], in_=attn_cache[:, 0, 1:POSITIONS].rearrange("l p h d -> p l (h d)"))
         with nc.allow_non_contiguous_dma(reason="32 mask values, one row for each head"):
-            nc.sync.dma_start(out=am_rows[0:HEADS, :], in_=attn_mask.rearrange("b l h -> h (b l)"))
+            nc.sync.dma_start(out=mask_rows[0:HEADS, 0 : BATCH * LAYERS], in_=attn_mask.rearrange("b l h -> h (b l)"))
+        nc.sync.dma_start(out=mask_rows[0:BATCH, MM_COL : MM_COL + N_MLP], in_=mlp_mask)
         modal = keep.tile([P, LAYERS, PACK], BF16)
         nc.sync.dma_start(
             out=modal[:], in_=modal_attention.rearrange("l h d -> l (h d)").rearrange("l (p t) -> p l t", t=PACK)
@@ -65,20 +59,19 @@ def tile_edgepruner_s_kernel(
         w = keep.tile([P, LAYERS, PACK, D_MODEL], BF16)
         w_dram = W_O.rearrange("l h d n -> l (h d) n")
         nc.sync.dma_start(out=w[:, 0], in_=w_dram[0].rearrange("(p j) n -> p j n", j=PACK))
-        nc.scalar.dma_start(out=small_rows[0:N_MLP, :], in_=modal_mlp)
-        nc.scalar.dma_start(out=small_rows[N_MLP : N_MLP + LAYERS, :], in_=post_bias)
-        with nc.allow_non_contiguous_dma(reason="six mask values, one row for each m"):
-            nc.scalar.dma_start(out=mask_rows[0:N_MLP, :], in_=mlp_mask.rearrange("b m -> m b"))
         table_warm = keep.tile([P, 1], BF16)
-        nc.scalar.copy(out=table_warm[:], in_=ones[:, 0:1])
-        nc.scalar.dma_start(out=mm_row[0:1, :], in_=mlp_mask.rearrange("b m -> (b m)").unsqueeze(0))
+        nc.scalar.copy(out=table_warm[:], in_=warm_in[:])
+        mlp_cols = keep.tile([P, N_MLP, NI], BF16)
+        nc.scalar.dma_start(out=mlp_cols[:], in_=modal_mlp.rearrange("m (q i) -> q m i", i=NI))
+        bias_cols = keep.tile([P, LAYERS, NI], BF16)
+        nc.scalar.dma_start(out=bias_cols[:], in_=post_bias.rearrange("l (q i) -> q l i", i=NI))
         caches = keep.tile([P, N_MLP, BATCH, D_MODEL], BF16)
-        nc.sync.dma_start(
-            out=caches[:, 0:2].rearrange("p m b n -> p (m b) n"),
-            in_=mlp_cache[0:2, :, 1:POSITIONS].rearrange("m b p n -> p (m b) n"),
-        )
+        nc.sync.dma_start(out=caches[:, 0], in_=mlp_cache[0, :, 1:POSITIONS].rearrange("b p n -> p b n"))
         nc.sync.dma_start(out=w[:, 1], in_=w_dram[1].rearrange("(p j) n -> p j n", j=PACK))
-        nc.sync.dma_start(out=caches[:, 2], in_=mlp_cache[2, :, 1:POSITIONS].rearrange("b p n -> p b n"))
+        nc.sync.dma_start(
+            out=caches[:, 1:3].rearrange("p m b n -> p (m b) n"),
+            in_=mlp_cache[1:3, :, 1:POSITIONS].rearrange("m b p n -> p (m b) n"),
+        )
         first_bf = keep.tile([BATCH, D_MODEL], BF16)
         nc.sync.dma_start(out=first_bf[:], in_=orig_in[:, 0, :])
 
@@ -86,22 +79,33 @@ def tile_edgepruner_s_kernel(
         nc.vector.tensor_copy(
             out=head_rows[:], in_=ident[:, 0:HEADS].unsqueeze(2).to_broadcast([P, HEADS, ROWS_PER_HEAD])
         )
-        am_spread = psum.tile([P, BATCH * LAYERS], F32, tag="x_t", bufs=3)
+        am_spread = psum.tile([P, BATCH, LAYERS], F32, tag="attn1")
         nc.tensor.matmul(
-            out=am_spread[:], lhsT=head_rows[:].rearrange("q h j -> q (h j)"), rhs=am_rows[:], start=True, stop=True
+            out=am_spread[:].rearrange("p b l -> p (b l)"),
+            lhsT=head_rows[:].rearrange("q h j -> q (h j)"),
+            rhs=mask_rows[:, 0 : BATCH * LAYERS],
+            start=True,
+            stop=True,
         )
-        am = keep.tile([P, BATCH, LAYERS], F32)
-        nc.vector.tensor_copy(out=am[:].rearrange("p b l -> p (b l)"), in_=am_spread[:])
-        one_minus_am = keep.tile([P, BATCH, LAYERS], F32)
-        nc.vector.tensor_scalar(
-            out=one_minus_am[:], in0=am[:], scalar1=-1.0, scalar2=1.0, op0=ALU.mult, op1=ALU.add
-        )
-        modal_term = keep.tile([P, BATCH, LAYERS, PACK], F32)
-        nc.vector.tensor_tensor(
-            out=modal_term[:],
-            in0=modal[:].unsqueeze(1).to_broadcast([P, BATCH, LAYERS, PACK]),
-            in1=one_minus_am[:].unsqueeze(3).to_broadcast([P, BATCH, LAYERS, PACK]),
-            op=ALU.mult,
+        mm_spread = psum.tile([P, BATCH, N_MLP], F32, tag="attn0")
+        for b in range(BATCH):
+            nc.tensor.matmul(
+                out=mm_spread[:, b, :],
+                lhsT=head_rows[:, b, 0:1].to_broadcast([P, P]),
+                rhs=mask_rows[:, MM_COL : MM_COL + N_MLP],
+                start=True,
+                stop=True,
+            )
+        mm = keep.tile([P, BATCH, N_MLP], F32)
+        nc.scalar.copy(out=mm[:], in_=mm_spread[:])
+        neg_modal = keep.tile([P, BATCH, LAYERS, PACK], F32)
+        nc.vector.scalar_tensor_tensor(
+            out=neg_modal[:],
+            in0=am_spread[:].unsqueeze(3).to_broadcast([P, BATCH, LAYERS, PACK]),
+            scalar=1.0,
+            in1=modal[:].unsqueeze(1).to_broadcast([P, BATCH, LAYERS, PACK]),
+            op0=ALU.subtract,
+            op1=ALU.mult,
         )
 
         a_bf = keep.tile([P, BATCH, LAYERS, P, PACK], BF16, align_bytes=64)
@@ -119,10 +123,10 @@ def tile_edgepruner_s_kernel(
             nc.vector.scalar_tensor_tensor(
                 out=a_bf[:, b, l],
                 in0=x_t[:].rearrange("p r u -> p (r u)").bitcast(BF16).rearrange("p (r t) -> p r t", t=PACK),
-                scalar=am[:, b, l : l + 1],
-                in1=modal_term[:, b, l, :].unsqueeze(1).to_broadcast([P, P, PACK]),
+                scalar=am_spread[:, b, l : l + 1],
+                in1=neg_modal[:, b, l, :].unsqueeze(1).to_broadcast([P, P, PACK]),
                 op0=ALU.mult,
-                op1=ALU.add,
+                op1=ALU.subtract,
             )
 
         def quantise_a(b):
@@ -139,31 +143,49 @@ def tile_edgepruner_s_kernel(
         blend(0, 0, x_t00)
         x_t11 = transpose_x(1, 1)
 
-        small_sums = psum.tile([P, N_CHUNKS * BATCH + BATCH * N_MLP], F32)
-        neg_const = small_sums[:, 0 : N_CHUNKS * BATCH].rearrange("p (c b) -> p c b", b=BATCH)
-        for c in range(N_CHUNKS):
-            chunk = small_rows[:, c * P : (c + 1) * P]
-            nc.tensor.matmul(out=neg_const[:, c, :], lhsT=chunk, rhs=minus_one[:], start=True, stop=False)
-            nc.tensor.matmul(out=neg_const[:, c, :], lhsT=chunk, rhs=mask_rows[:], start=False, stop=True)
-        nc.tensor.matmul(out=small_sums[:, N_CHUNKS * BATCH :], lhsT=ones[:], rhs=mm_row[:], start=True, stop=True)
+        def add_small(name, shape, in0, in1, op=ALU.add):
+            total = keep.tile(shape, F32, name=name)
+            nc.gpsimd.tensor_tensor(out=total[:], in0=in0, in1=in1, op=op)
+            return total
+
+        one_minus_mm = keep.tile([P, BATCH, N_MLP], F32)
+        nc.gpsimd.tensor_scalar(out=one_minus_mm[:], in0=mm[:], scalar1=-1.0, scalar2=1.0, op0=ALU.mult, op1=ALU.add)
+        weighted = add_small(
+            "weighted",
+            [P, BATCH, N_MLP, NI],
+            mlp_cols[:].unsqueeze(1).to_broadcast([P, BATCH, N_MLP, NI]),
+            one_minus_mm[:].unsqueeze(3).to_broadcast([P, BATCH, N_MLP, NI]),
+            ALU.mult,
+        )
+        weighted_01 = add_small("weighted_01", [P, BATCH, NI], weighted[:, :, 0, :], weighted[:, :, 1, :])
+        weighted_012 = add_small("weighted_012", [P, BATCH, NI], weighted_01[:], weighted[:, :, 2, :])
+        bias_sum = add_small("bias_sum", [P, NI], bias_cols[:, 0, :], bias_cols[:, 1, :])
+        const_col = add_small(
+            "const_col", [P, BATCH, NI], weighted_012[:], bias_sum[:].unsqueeze(1).to_broadcast([P, BATCH, NI])
+        )
+
+        diag = keep.tile([P, P], BF16)
+        nc.gpsimd.tensor_scalar(
+            out=diag[:], in0=ident[:], scalar1=mm[:, 0, 0:1], scalar2=0.0, op0=ALU.mult, op1=ALU.add
+        )
 
         blend(0, 1, x_t01)
         blend(1, 0, x_t10)
         quantise_a(0)
         blend(1, 1, x_t11)
-        small_sb = keep.tile([P, N_CHUNKS * BATCH + BATCH * N_MLP], F32)
-        nc.vector.tensor_copy(out=small_sb[:], in_=small_sums[:])
-        neg_const_col = small_sb[:, 0 : N_CHUNKS * BATCH].rearrange("p (c b) -> p c b", b=BATCH)
-        mm = small_sb[:, N_CHUNKS * BATCH :].rearrange("p (b m) -> p b m", m=N_MLP)
 
-        neg_const_all = []
-        for b in range(BATCH):
-            spread = psum.tile([P, D_MODEL], F32, name="neg_const_all%d" % b)
-            for c in range(N_CHUNKS):
-                nc.tensor.transpose(
-                    spread[:, c * P : (c + 1) * P], neg_const_col[:, c, b : b + 1].to_broadcast([P, P]), ident[:]
+        const_all = [psum.tile([P, D_MODEL], F32, name="const_all%d" % b) for b in range(BATCH)]
+        for b in reversed(range(BATCH)):
+            for i in range(NI):
+                nc.tensor.matmul(
+                    out=const_all[b][:].rearrange("p (q i) -> p i q", i=NI)[:, i, :],
+                    lhsT=const_col[:, b, i : i + 1].to_broadcast([P, P]),
+                    rhs=ident[:],
+                    is_transpose=True,
+                    start=(b > 0 or i == 0),
+                    stop=(b > 0),
                 )
-            neg_const_all.append(spread)
+        nc.tensor.matmul(out=const_all[0][:], lhsT=diag[:], rhs=caches[:, 0, 0, :], start=False, stop=True)
 
         w_grouped = keep.tile([P, LAYERS, D_MODEL, PACK], BF16, align_bytes=64)
         w_codes = keep.tile([P, LAYERS, D_MODEL], U32, align_bytes=64)
@@ -185,7 +207,7 @@ def tile_edgepruner_s_kernel(
                 in_=w_grouped[:, l].rearrange("p n j -> p (n j)"),
             )
 
-        attn = [psum.tile([P, D_MODEL], F32, name="attn%d" % b) for b in range(BATCH)]
+        attn = [psum.tile([P, D_MODEL], F32, tag="attn%d" % b, name="attn_sum%d" % b) for b in range(BATCH)]
 
         def mx_passes(l):
             for b in range(BATCH):
@@ -206,16 +228,15 @@ def tile_edgepruner_s_kernel(
                 out=mlp[b][:],
                 in0=caches[:, m, b, :],
                 scalar=mm[:, b, m : m + 1],
-                in1=(neg_const_all[b][:] if m == 0 else mlp[b][:]),
+                in1=(const_all[b][:] if m == FIRST_M[b] else mlp[b][:]),
                 op0=ALU.mult,
-                op1=(ALU.subtract if m == 0 else ALU.add),
+                op1=ALU.add,
             )
 
         quantise_a(1)
+        add_cache(1, 0)
         quantise_w(0)
         mx_passes(0)
-        add_cache(0, 0)
-        add_cache(1, 0)
         add_cache(0, 1)
         add_cache(1, 1)
         quantise_w(1)

@@ -10,12 +10,14 @@ U8 = mybir.dt.uint8
 FP8X4 = mybir.dt.float8_e4m3fn_x4
 ALU = mybir.AluOpType
 AX = mybir.AxisListType
+ACT = mybir.ActivationFunctionType
 
 LAYERS, BATCH, POSITIONS, HEADS, D_HEAD, D_MODEL = 2, 2, 129, 8, 64, 512
 N_MLP = LAYERS + 1
 P = 128
 PACK = 4
 K_PASS = P * PACK
+HALF = D_MODEL // 2
 NI = D_MODEL // P
 FIRST_M = (1, 0)
 MM_COL = 16
@@ -55,23 +57,25 @@ def tile_edgepruner_s_kernel(
         nc.sync.dma_start(
             out=modal[:], in_=modal_attention.rearrange("l h d -> l (h d)").rearrange("l (p t) -> p l t", t=PACK)
         )
+        mlp_cols = keep.tile([P, N_MLP, NI], BF16)
+        nc.sync.dma_start(out=mlp_cols[:], in_=modal_mlp.rearrange("m (q i) -> q m i", i=NI))
+        bias_cols = keep.tile([P, LAYERS, NI], BF16)
+        nc.sync.dma_start(out=bias_cols[:], in_=post_bias.rearrange("l (q i) -> q l i", i=NI))
         nc.sync.dma_start(out=x[:, 1], in_=attn_cache[:, 1, 1:POSITIONS].rearrange("l p h d -> p l (h d)"))
         w = keep.tile([P, LAYERS, PACK, D_MODEL], BF16)
         w_dram = W_O.rearrange("l h d n -> l (h d) n")
         nc.sync.dma_start(out=w[:, 0], in_=w_dram[0].rearrange("(p j) n -> p j n", j=PACK))
         table_warm = keep.tile([P, 1], BF16)
         nc.scalar.copy(out=table_warm[:], in_=warm_in[:])
-        mlp_cols = keep.tile([P, N_MLP, NI], BF16)
-        nc.scalar.dma_start(out=mlp_cols[:], in_=modal_mlp.rearrange("m (q i) -> q m i", i=NI))
-        bias_cols = keep.tile([P, LAYERS, NI], BF16)
-        nc.scalar.dma_start(out=bias_cols[:], in_=post_bias.rearrange("l (q i) -> q l i", i=NI))
         caches = keep.tile([P, N_MLP, BATCH, D_MODEL], BF16)
-        nc.sync.dma_start(out=caches[:, 0], in_=mlp_cache[0, :, 1:POSITIONS].rearrange("b p n -> p b n"))
+
+        def load_cache(m):
+            nc.sync.dma_start(out=caches[:, m], in_=mlp_cache[m, :, 1:POSITIONS].rearrange("b p n -> p b n"))
+
+        load_cache(0)
+        load_cache(1)
         nc.sync.dma_start(out=w[:, 1], in_=w_dram[1].rearrange("(p j) n -> p j n", j=PACK))
-        nc.sync.dma_start(
-            out=caches[:, 1:3].rearrange("p m b n -> p (m b) n"),
-            in_=mlp_cache[1:3, :, 1:POSITIONS].rearrange("m b p n -> p (m b) n"),
-        )
+        load_cache(2)
         first_bf = keep.tile([BATCH, D_MODEL], BF16)
         nc.sync.dma_start(out=first_bf[:], in_=orig_in[:, 0, :])
 
@@ -87,7 +91,15 @@ def tile_edgepruner_s_kernel(
             start=True,
             stop=True,
         )
-        mm_spread = psum.tile([P, BATCH, N_MLP], F32, tag="attn0")
+        spread_2 = psum.tile([P, BATCH * N_MLP + 1], F32, tag="attn0")
+        mm_spread = spread_2[:, 0 : BATCH * N_MLP].rearrange("p (b m) -> p b m", m=N_MLP)
+        nc.tensor.matmul(
+            out=spread_2[:, BATCH * N_MLP :],
+            lhsT=head_rows[:].rearrange("q h j -> q (h j)"),
+            rhs=mask_rows[:, 1:2],
+            start=True,
+            stop=True,
+        )
         for b in range(BATCH):
             nc.tensor.matmul(
                 out=mm_spread[:, b, :],
@@ -96,8 +108,12 @@ def tile_edgepruner_s_kernel(
                 start=True,
                 stop=True,
             )
+        one_minus_mm = keep.tile([P, BATCH, N_MLP], F32)
+        nc.scalar.activation(out=one_minus_mm[:], in_=mm_spread, func=ACT.Identity, scale=-1.0, bias=1.0)
         mm = keep.tile([P, BATCH, N_MLP], F32)
-        nc.scalar.copy(out=mm[:], in_=mm_spread[:])
+        nc.scalar.copy(out=mm[:], in_=mm_spread)
+        neg_am_01 = keep.tile([P, 1], F32)
+        nc.scalar.mul(neg_am_01[:], spread_2[:, BATCH * N_MLP :], -1.0)
         neg_modal = keep.tile([P, BATCH, LAYERS, PACK], F32)
         nc.vector.scalar_tensor_tensor(
             out=neg_modal[:],
@@ -140,38 +156,50 @@ def tile_edgepruner_s_kernel(
         x_t01 = transpose_x(0, 1)
         x_t10 = transpose_x(1, 0)
 
+        neg_a_01 = keep.tile([P, PACK, P], BF16)
+        for t in range(PACK):
+            nc.scalar.activation(
+                out=neg_a_01[:, t, :],
+                in_=x_t01[:].rearrange("p r u -> p (r u)").bitcast(BF16).rearrange("p (r t) -> p t r", t=PACK)[:, t, :],
+                func=ACT.Identity,
+                scale=neg_am_01[:],
+                bias=neg_modal[:, 0, 1, t : t + 1],
+            )
         blend(0, 0, x_t00)
         x_t11 = transpose_x(1, 1)
 
-        def add_small(name, shape, in0, in1, op=ALU.add):
-            total = keep.tile(shape, F32, name=name)
-            nc.gpsimd.tensor_tensor(out=total[:], in0=in0, in1=in1, op=op)
-            return total
-
-        one_minus_mm = keep.tile([P, BATCH, N_MLP], F32)
-        nc.gpsimd.tensor_scalar(out=one_minus_mm[:], in0=mm[:], scalar1=-1.0, scalar2=1.0, op0=ALU.mult, op1=ALU.add)
-        weighted = add_small(
-            "weighted",
-            [P, BATCH, N_MLP, NI],
-            mlp_cols[:].unsqueeze(1).to_broadcast([P, BATCH, N_MLP, NI]),
-            one_minus_mm[:].unsqueeze(3).to_broadcast([P, BATCH, N_MLP, NI]),
-            ALU.mult,
+        const_terms = keep.tile([P, BATCH, N_MLP + 1, NI], F32)
+        nc.gpsimd.tensor_tensor(
+            out=const_terms[:, :, N_MLP, :],
+            in0=bias_cols[:, 0, :].unsqueeze(1).to_broadcast([P, BATCH, NI]),
+            in1=bias_cols[:, 1, :].unsqueeze(1).to_broadcast([P, BATCH, NI]),
+            op=ALU.add,
         )
-        weighted_01 = add_small("weighted_01", [P, BATCH, NI], weighted[:, :, 0, :], weighted[:, :, 1, :])
-        weighted_012 = add_small("weighted_012", [P, BATCH, NI], weighted_01[:], weighted[:, :, 2, :])
-        bias_sum = add_small("bias_sum", [P, NI], bias_cols[:, 0, :], bias_cols[:, 1, :])
-        const_col = add_small(
-            "const_col", [P, BATCH, NI], weighted_012[:], bias_sum[:].unsqueeze(1).to_broadcast([P, BATCH, NI])
+        nc.gpsimd.tensor_tensor(
+            out=const_terms[:, :, 0:N_MLP, :],
+            in0=mlp_cols[:].unsqueeze(1).to_broadcast([P, BATCH, N_MLP, NI]),
+            in1=one_minus_mm[:].unsqueeze(3).to_broadcast([P, BATCH, N_MLP, NI]),
+            op=ALU.mult,
+        )
+        const_col = keep.tile([P, BATCH, NI], F32)
+        nc.vector.tensor_reduce(
+            out=const_col[:], in_=const_terms[:].rearrange("p b s i -> p b i s"), axis=AX.X, op=ALU.add
         )
 
+        nc.gpsimd.tensor_scalar(
+            out=a_bf[:, 0, 1],
+            in0=neg_a_01[:].rearrange("p t r -> p r t"),
+            scalar1=-1.0,
+            scalar2=0.0,
+            op0=ALU.mult,
+            op1=ALU.add,
+        )
         diag = keep.tile([P, P], BF16)
         nc.gpsimd.tensor_scalar(
             out=diag[:], in0=ident[:], scalar1=mm[:, 0, 0:1], scalar2=0.0, op0=ALU.mult, op1=ALU.add
         )
 
-        blend(0, 1, x_t01)
         blend(1, 0, x_t10)
-        quantise_a(0)
         blend(1, 1, x_t11)
 
         const_all = [psum.tile([P, D_MODEL], F32, name="const_all%d" % b) for b in range(BATCH)]
@@ -190,33 +218,41 @@ def tile_edgepruner_s_kernel(
         w_grouped = keep.tile([P, LAYERS, D_MODEL, PACK], BF16, align_bytes=64)
         w_codes = keep.tile([P, LAYERS, D_MODEL], U32, align_bytes=64)
         w_scales = keep.tile([P, LAYERS, D_MODEL], U8, align_bytes=64)
-        for l in range(LAYERS):
+        def regroup(l, first_n, end_n):
             nc.scalar.copy(
-                out=w_grouped[:, l].rearrange("p (g i) j -> p g j i", i=4),
-                in_=w[:, l].rearrange("p j (g i) -> p g j i", i=4),
+                out=w_grouped[:, l, first_n:end_n].rearrange("p (g i) j -> p g j i", i=4),
+                in_=w[:, l, :, first_n:end_n].rearrange("p j (g i) -> p g j i", i=4),
             )
+
+        regroup(0, 0, D_MODEL)
+        for half in range(2):
+            regroup(1, half * HALF, (half + 1) * HALF)
 
         first = keep.tile([BATCH, D_MODEL], F32)
         nc.scalar.copy(out=first[:], in_=first_bf[:])
         nc.sync.dma_start(out=out[:, 0, :], in_=first[:])
 
-        def quantise_w(l):
+        def quantise_w(l, first_n, end_n):
             nc.vector.quantize_mx(
-                out=w_codes[:, l].bitcast(FP8X4),
-                scales=w_scales[:, l],
-                in_=w_grouped[:, l].rearrange("p n j -> p (n j)"),
+                out=w_codes[:, l, first_n:end_n].bitcast(FP8X4),
+                scales=w_scales[:, l, first_n:end_n],
+                in_=w_grouped[:, l, first_n:end_n].rearrange("p n j -> p (n j)"),
             )
 
-        attn = [psum.tile([P, D_MODEL], F32, tag="attn%d" % b, name="attn_sum%d" % b) for b in range(BATCH)]
+        attn = [
+            [psum.tile([P, HALF], F32, tag="attn%d" % b, name="attn_a%d" % b) for b in range(BATCH)],
+            [psum.tile([P, HALF], F32, tag="x_t", bufs=3, name="attn_b%d" % b) for b in range(BATCH)],
+        ]
 
-        def mx_passes(l):
+        def mx_passes(l, half):
+            n = slice(half * HALF, (half + 1) * HALF)
             for b in range(BATCH):
                 nc.tensor.matmul_mx(
-                    out=attn[b][:],
+                    out=attn[half][b][:],
                     lhsT=a_codes[:, b, l].bitcast(FP8X4),
                     lhsT_scale=a_scales[:, b, l],
-                    rhs=w_codes[:, l].bitcast(FP8X4),
-                    rhs_scale=w_scales[:, l],
+                    rhs=w_codes[:, l, n].bitcast(FP8X4),
+                    rhs_scale=w_scales[:, l, n],
                     start=(l == 0),
                     stop=(l == LAYERS - 1),
                 )
@@ -233,17 +269,27 @@ def tile_edgepruner_s_kernel(
                 op1=ALU.add,
             )
 
-        quantise_a(1)
+        def finish(b, half):
+            n = slice(half * HALF, (half + 1) * HALF)
+            result = keep.tile([P, HALF], F32, name="result%d%d" % (b, half))
+            nc.vector.tensor_tensor(out=result[:], in0=attn[half][b][:], in1=mlp[b][:, n], op=ALU.add)
+            nc.sync.dma_start(out=out[b, 1:POSITIONS, n], in_=result[:])
+
         add_cache(1, 0)
-        quantise_w(0)
-        mx_passes(0)
-        add_cache(0, 1)
+        quantise_a(1)
         add_cache(1, 1)
-        quantise_w(1)
-        mx_passes(1)
-        add_cache(0, 2)
+        quantise_a(0)
+        quantise_w(0, 0, D_MODEL)
+        mx_passes(0, 0)
+        mx_passes(0, 1)
+        add_cache(0, 1)
+        quantise_w(1, 0, HALF)
+        mx_passes(1, 0)
         add_cache(1, 2)
-        for b in range(BATCH):
-            result = keep.tile([P, D_MODEL], F32, name="result%d" % b)
-            nc.vector.tensor_tensor(out=result[:], in0=attn[b][:], in1=mlp[b][:], op=ALU.add)
-            nc.sync.dma_start(out=out[b, 1:POSITIONS, :], in_=result[:])
+        add_cache(0, 2)
+        quantise_w(1, HALF, D_MODEL)
+        mx_passes(1, 1)
+        finish(1, 0)
+        finish(0, 0)
+        finish(1, 1)
+        finish(0, 1)

@@ -19,7 +19,7 @@ PACK = 4
 K_PASS = P * PACK
 HALF = D_MODEL // 2
 NI = D_MODEL // P
-FIRST_M = (1, 0)
+N_IDLE = 9
 MM_COL = 16
 ROWS_PER_HEAD = D_HEAD // PACK
 
@@ -47,6 +47,11 @@ def tile_edgepruner_s_kernel(
         make_identity(nc, ident[:], nomemset=True)
         warm_in = keep.tile([P, 1], BF16)
         nc.vector.memset(warm_in[:], 0.0)
+        zeros = keep.tile([P, P], F32)
+        nc.vector.memset(zeros[:], 0.0)
+        idle_out = psum.tile([P, P], F32, tag="const_all1")
+        for i in range(N_IDLE):
+            nc.tensor.transpose(idle_out[:], zeros[:], zeros[:])
 
         x = keep.tile([P, BATCH, LAYERS, K_PASS], BF16)
         nc.sync.dma_start(out=x[:, 0], in_=attn_cache[:, 0, 1:POSITIONS].rearrange("l p h d -> p l (h d)"))
@@ -59,9 +64,9 @@ def tile_edgepruner_s_kernel(
         )
         mlp_cols = keep.tile([P, N_MLP, NI], BF16)
         nc.sync.dma_start(out=mlp_cols[:], in_=modal_mlp.rearrange("m (q i) -> q m i", i=NI))
+        nc.sync.dma_start(out=x[:, 1], in_=attn_cache[:, 1, 1:POSITIONS].rearrange("l p h d -> p l (h d)"))
         bias_cols = keep.tile([P, LAYERS, NI], BF16)
         nc.sync.dma_start(out=bias_cols[:], in_=post_bias.rearrange("l (q i) -> q l i", i=NI))
-        nc.sync.dma_start(out=x[:, 1], in_=attn_cache[:, 1, 1:POSITIONS].rearrange("l p h d -> p l (h d)"))
         w = keep.tile([P, LAYERS, PACK, D_MODEL], BF16)
         w_dram = W_O.rearrange("l h d n -> l (h d) n")
         nc.sync.dma_start(out=w[:, 0], in_=w_dram[0].rearrange("(p j) n -> p j n", j=PACK))
@@ -114,6 +119,9 @@ def tile_edgepruner_s_kernel(
         nc.scalar.copy(out=mm[:], in_=mm_spread)
         neg_am_01 = keep.tile([P, 1], F32)
         nc.scalar.mul(neg_am_01[:], spread_2[:, BATCH * N_MLP :], -1.0)
+        diag = keep.tile([P, 2, P], BF16)
+        for m in range(2):
+            nc.scalar.activation(out=diag[:, m, :], in_=ident[:], func=ACT.Copy, scale=mm[:, 0, m : m + 1])
         neg_modal = keep.tile([P, BATCH, LAYERS, PACK], F32)
         nc.vector.scalar_tensor_tensor(
             out=neg_modal[:],
@@ -130,7 +138,7 @@ def tile_edgepruner_s_kernel(
 
         def transpose_x(b, l):
             words = x[:, b, l, :].bitcast(F32).rearrange("p (w u) -> p u w", u=2)
-            x_t = psum.tile([P, P, 2], F32, tag="x_t", bufs=3, name="x_t%d%d" % (b, l))
+            x_t = psum.tile([P, P, 2], F32, tag="x_t", bufs=4, name="x_t%d%d" % (b, l))
             for u in range(2):
                 nc.tensor.transpose(x_t[:, :, u], words[:, u, :], ident[:])
             return x_t
@@ -170,22 +178,17 @@ def tile_edgepruner_s_kernel(
 
         const_terms = keep.tile([P, BATCH, N_MLP + 1, NI], F32)
         nc.gpsimd.tensor_tensor(
-            out=const_terms[:, :, N_MLP, :],
-            in0=bias_cols[:, 0, :].unsqueeze(1).to_broadcast([P, BATCH, NI]),
-            in1=bias_cols[:, 1, :].unsqueeze(1).to_broadcast([P, BATCH, NI]),
-            op=ALU.add,
-        )
-        nc.gpsimd.tensor_tensor(
             out=const_terms[:, :, 0:N_MLP, :],
             in0=mlp_cols[:].unsqueeze(1).to_broadcast([P, BATCH, N_MLP, NI]),
             in1=one_minus_mm[:].unsqueeze(3).to_broadcast([P, BATCH, N_MLP, NI]),
             op=ALU.mult,
         )
-        const_col = keep.tile([P, BATCH, NI], F32)
-        nc.vector.tensor_reduce(
-            out=const_col[:], in_=const_terms[:].rearrange("p b s i -> p b i s"), axis=AX.X, op=ALU.add
+        nc.gpsimd.tensor_tensor(
+            out=const_terms[:, :, N_MLP, :],
+            in0=bias_cols[:, 0, :].unsqueeze(1).to_broadcast([P, BATCH, NI]),
+            in1=bias_cols[:, 1, :].unsqueeze(1).to_broadcast([P, BATCH, NI]),
+            op=ALU.add,
         )
-
         nc.gpsimd.tensor_scalar(
             out=a_bf[:, 0, 1],
             in0=neg_a_01[:].rearrange("p t r -> p r t"),
@@ -194,15 +197,14 @@ def tile_edgepruner_s_kernel(
             op0=ALU.mult,
             op1=ALU.add,
         )
-        diag = keep.tile([P, P], BF16)
-        nc.gpsimd.tensor_scalar(
-            out=diag[:], in0=ident[:], scalar1=mm[:, 0, 0:1], scalar2=0.0, op0=ALU.mult, op1=ALU.add
+        const_col = keep.tile([P, BATCH, NI], F32)
+        nc.vector.tensor_reduce(
+            out=const_col[:], in_=const_terms[:].rearrange("p b s i -> p b i s"), axis=AX.X, op=ALU.add
         )
-
         blend(1, 0, x_t10)
         blend(1, 1, x_t11)
 
-        const_all = [psum.tile([P, D_MODEL], F32, name="const_all%d" % b) for b in range(BATCH)]
+        const_all = [psum.tile([P, D_MODEL], F32, tag="const_all%d" % b, name="const_sum%d" % b) for b in range(BATCH)]
         for b in reversed(range(BATCH)):
             for i in range(NI):
                 nc.tensor.matmul(
@@ -213,7 +215,9 @@ def tile_edgepruner_s_kernel(
                     start=(b > 0 or i == 0),
                     stop=(b > 0),
                 )
-        nc.tensor.matmul(out=const_all[0][:], lhsT=diag[:], rhs=caches[:, 0, 0, :], start=False, stop=True)
+        half_a, half_b = slice(0, HALF), slice(HALF, D_MODEL)
+        nc.tensor.matmul(out=const_all[0][:], lhsT=diag[:, 0, :], rhs=caches[:, 0, 0, :], start=False, stop=False)
+        nc.tensor.matmul(out=const_all[0][:, half_a], lhsT=diag[:, 1, :], rhs=caches[:, 1, 0, half_a], start=False, stop=True)
 
         w_grouped = keep.tile([P, LAYERS, D_MODEL, PACK], BF16, align_bytes=64)
         w_codes = keep.tile([P, LAYERS, D_MODEL], U32, align_bytes=64)
@@ -241,7 +245,7 @@ def tile_edgepruner_s_kernel(
 
         attn = [
             [psum.tile([P, HALF], F32, tag="attn%d" % b, name="attn_a%d" % b) for b in range(BATCH)],
-            [psum.tile([P, HALF], F32, tag="x_t", bufs=3, name="attn_b%d" % b) for b in range(BATCH)],
+            [psum.tile([P, HALF], F32, tag="x_t", bufs=4, name="attn_b%d" % b) for b in range(BATCH)],
         ]
 
         def mx_passes(l, half):
@@ -259,12 +263,12 @@ def tile_edgepruner_s_kernel(
 
         mlp = [keep.tile([P, D_MODEL], F32, name="mlp%d" % b) for b in range(BATCH)]
 
-        def add_cache(b, m):
+        def add_cache(b, m, earlier, n=slice(0, D_MODEL)):
             nc.vector.scalar_tensor_tensor(
-                out=mlp[b][:],
-                in0=caches[:, m, b, :],
+                out=mlp[b][:, n],
+                in0=caches[:, m, b, n],
                 scalar=mm[:, b, m : m + 1],
-                in1=(const_all[b][:] if m == FIRST_M[b] else mlp[b][:]),
+                in1=earlier[:, n],
                 op0=ALU.mult,
                 op1=ALU.add,
             )
@@ -275,18 +279,19 @@ def tile_edgepruner_s_kernel(
             nc.vector.tensor_tensor(out=result[:], in0=attn[half][b][:], in1=mlp[b][:, n], op=ALU.add)
             nc.sync.dma_start(out=out[b, 1:POSITIONS, n], in_=result[:])
 
-        add_cache(1, 0)
+        add_cache(1, 0, const_all[1])
         quantise_a(1)
-        add_cache(1, 1)
+        add_cache(1, 1, mlp[1])
         quantise_a(0)
+        add_cache(0, 1, const_all[0], half_b)
         quantise_w(0, 0, D_MODEL)
         mx_passes(0, 0)
         mx_passes(0, 1)
-        add_cache(0, 1)
+        add_cache(1, 2, mlp[1])
         quantise_w(1, 0, HALF)
         mx_passes(1, 0)
-        add_cache(1, 2)
-        add_cache(0, 2)
+        add_cache(0, 2, const_all[0], half_a)
+        add_cache(0, 2, mlp[0], half_b)
         quantise_w(1, HALF, D_MODEL)
         mx_passes(1, 1)
         finish(1, 0)

from contextlib import ExitStack

import concourse.mybir as mybir
from concourse.masks import make_identity

BF16 = mybir.dt.bfloat16
F32 = mybir.dt.float32
U32 = mybir.dt.uint32
U8 = mybir.dt.uint8
FP8X4 = mybir.dt.float8_e4m3fn_x4
ALU = mybir.AluOpType
AX = mybir.AxisListType
ACT = mybir.ActivationFunctionType

LAYERS, BATCH, POSITIONS, HEADS, D_HEAD, D_MODEL = 2, 2, 129, 8, 64, 512
N_MLP = LAYERS + 1
P = 128
PACK = 4
K_PASS = P * PACK
HALF = D_MODEL // 2
NI = D_MODEL // P
N_IDLE = 9
MM_COL = 16
ROWS_PER_HEAD = D_HEAD // PACK

FLOPS = 2 * BATCH * P * LAYERS * K_PASS * D_MODEL
BYTES = (
    2 * (LAYERS * BATCH * P * K_PASS + N_MLP * BATCH * P * D_MODEL + LAYERS * K_PASS * D_MODEL)
    + 2 * (BATCH * N_MLP + BATCH * LAYERS * HEADS + LAYERS * K_PASS + (N_MLP + LAYERS + BATCH) * D_MODEL)
    + 4 * BATCH * POSITIONS * D_MODEL
)


def tile_edgepruner_s_kernel(
    tc, attn_cache, mlp_cache, mlp_mask, attn_mask, modal_attention, modal_mlp, W_O, post_bias, orig_in, out
):
    nc = tc.nc
    with ExitStack() as ctx:
        keep = ctx.enter_context(tc.tile_pool(name="keep", bufs=1))
        psum = ctx.enter_context(tc.psum_pool(name="psum", bufs=1))
        ctx.enter_context(tc.manual_schedule())

        mask_rows = keep.tile([P, MM_COL + N_MLP], BF16)
        nc.gpsimd.memset(mask_rows[:], 0.0)
        ident = keep.tile([P, P], F32)
        nc.vector.memset(ident[:], 0.0)
        make_identity(nc, ident[:], nomemset=True)
        warm_in = keep.tile([P, 1], BF16)
        nc.vector.memset(warm_in[:], 0.0)
        zeros = keep.tile([P, P], F32)
        nc.vector.memset(zeros[:], 0.0)
        idle_out = psum.tile([P, P], F32, tag="const_all1")
        for i in range(N_IDLE):
            nc.tensor.transpose(idle_out[:], zeros[:], zeros[:])

        x = keep.tile([P, BATCH, LAYERS, K_PASS], BF16)
        nc.sync.dma_start(out=x[:, 0], in_=attn_cache[:, 0, 1:POSITIONS].rearrange("l p h d -> p l (h d)"))
        with nc.allow_non_contiguous_dma(reason="32 mask values, one row for each head"):
            nc.sync.dma_start(out=mask_rows[0:HEADS, 0 : BATCH * LAYERS], in_=attn_mask.rearrange("b l h -> h (b l)"))
        nc.sync.dma_start(out=mask_rows[0:BATCH, MM_COL : MM_COL + N_MLP], in_=mlp_mask)
        modal = keep.tile([P, LAYERS, PACK], BF16)
        nc.sync.dma_start(
            out=modal[:], in_=modal_attention.rearrange("l h d -> l (h d)").rearrange("l (p t) -> p l t", t=PACK)
        )
        mlp_cols = keep.tile([P, N_MLP, NI], BF16)
        nc.sync.dma_start(out=mlp_cols[:], in_=modal_mlp.rearrange("m (q i) -> q m i", i=NI))
        nc.sync.dma_start(out=x[:, 1], in_=attn_cache[:, 1, 1:POSITIONS].rearrange("l p h d -> p l (h d)"))
        bias_cols = keep.tile([P, LAYERS, NI], BF16)
        nc.sync.dma_start(out=bias_cols[:], in_=post_bias.rearrange("l (q i) -> q l i", i=NI))
        w = keep.tile([P, LAYERS, PACK, D_MODEL], BF16)
        w_dram = W_O.rearrange("l h d n -> l (h d) n")
        nc.sync.dma_start(out=w[:, 0], in_=w_dram[0].rearrange("(p j) n -> p j n", j=PACK))
        table_warm = keep.tile([P, 1], BF16)
        nc.scalar.copy(out=table_warm[:], in_=warm_in[:])
        caches = keep.tile([P, N_MLP, BATCH, D_MODEL], BF16)

        def load_cache(m):
            nc.sync.dma_start(out=caches[:, m], in_=mlp_cache[m, :, 1:POSITIONS].rearrange("b p n -> p b n"))

        load_cache(0)
        load_cache(1)
        nc.sync.dma_start(out=w[:, 1], in_=w_dram[1].rearrange("(p j) n -> p j n", j=PACK))
        load_cache(2)
        first_bf = keep.tile([BATCH, D_MODEL], BF16)
        nc.sync.dma_start(out=first_bf[:], in_=orig_in[:, 0, :])

        head_rows = keep.tile([P, HEADS, ROWS_PER_HEAD], BF16)
        nc.vector.tensor_copy(
            out=head_rows[:], in_=ident[:, 0:HEADS].unsqueeze(2).to_broadcast([P, HEADS, ROWS_PER_HEAD])
        )
        am_spread = psum.tile([P, BATCH, LAYERS], F32, tag="attn1")
        nc.tensor.matmul(
            out=am_spread[:].rearrange("p b l -> p (b l)"),
            lhsT=head_rows[:].rearrange("q h j -> q (h j)"),
            rhs=mask_rows[:, 0 : BATCH * LAYERS],
            start=True,
            stop=True,
        )
        spread_2 = psum.tile([P, BATCH * N_MLP + 1], F32, tag="attn0")
        mm_spread = spread_2[:, 0 : BATCH * N_MLP].rearrange("p (b m) -> p b m", m=N_MLP)
        nc.tensor.matmul(
            out=spread_2[:, BATCH * N_MLP :],
            lhsT=head_rows[:].rearrange("q h j -> q (h j)"),
            rhs=mask_rows[:, 1:2],
            start=True,
            stop=True,
        )
        for b in range(BATCH):
            nc.tensor.matmul(
                out=mm_spread[:, b, :],
                lhsT=head_rows[:, b, 0:1].to_broadcast([P, P]),
                rhs=mask_rows[:, MM_COL : MM_COL + N_MLP],
                start=True,
                stop=True,
            )
        one_minus_mm = keep.tile([P, BATCH, N_MLP], F32)
        nc.scalar.activation(out=one_minus_mm[:], in_=mm_spread, func=ACT.Identity, scale=-1.0, bias=1.0)
        mm = keep.tile([P, BATCH, N_MLP], F32)
        nc.scalar.copy(out=mm[:], in_=mm_spread)
        neg_am_01 = keep.tile([P, 1], F32)
        nc.scalar.mul(neg_am_01[:], spread_2[:, BATCH * N_MLP :], -1.0)
        diag = keep.tile([P, 2, P], BF16)
        for m in range(2):
            nc.scalar.activation(out=diag[:, m, :], in_=ident[:], func=ACT.Copy, scale=mm[:, 0, m : m + 1])
        neg_modal = keep.tile([P, BATCH, LAYERS, PACK], F32)
        nc.vector.scalar_tensor_tensor(
            out=neg_modal[:],
            in0=am_spread[:].unsqueeze(3).to_broadcast([P, BATCH, LAYERS, PACK]),
            scalar=1.0,
            in1=modal[:].unsqueeze(1).to_broadcast([P, BATCH, LAYERS, PACK]),
            op0=ALU.subtract,
            op1=ALU.mult,
        )

        a_bf = keep.tile([P, BATCH, LAYERS, P, PACK], BF16, align_bytes=64)
        a_codes = keep.tile([P, BATCH, LAYERS, P], U32, align_bytes=64)
        a_scales = keep.tile([P, BATCH, LAYERS, P], U8, align_bytes=64)

        def transpose_x(b, l):
            words = x[:, b, l, :].bitcast(F32).rearrange("p (w u) -> p u w", u=2)
            x_t = psum.tile([P, P, 2], F32, tag="x_t", bufs=4, name="x_t%d%d" % (b, l))
            for u in range(2):
                nc.tensor.transpose(x_t[:, :, u], words[:, u, :], ident[:])
            return x_t

        def blend(b, l, x_t):
            nc.vector.scalar_tensor_tensor(
                out=a_bf[:, b, l],
                in0=x_t[:].rearrange("p r u -> p (r u)").bitcast(BF16).rearrange("p (r t) -> p r t", t=PACK),
                scalar=am_spread[:, b, l : l + 1],
                in1=neg_modal[:, b, l, :].unsqueeze(1).to_broadcast([P, P, PACK]),
                op0=ALU.mult,
                op1=ALU.subtract,
            )

        def quantise_a(b):
            nc.vector.quantize_mx(
                out=a_codes[:, b].rearrange("p l r -> p (l r)").bitcast(FP8X4),
                scales=a_scales[:, b].rearrange("p l r -> p (l r)"),
                in_=a_bf[:, b].rearrange("p l r t -> p (l r t)"),
            )

        x_t00 = transpose_x(0, 0)
        x_t01 = transpose_x(0, 1)
        x_t10 = transpose_x(1, 0)

        neg_a_01 = keep.tile([P, PACK, P], BF16)
        for t in range(PACK):
            nc.scalar.activation(
                out=neg_a_01[:, t, :],
                in_=x_t01[:].rearrange("p r u -> p (r u)").bitcast(BF16).rearrange("p (r t) -> p t r", t=PACK)[:, t, :],
                func=ACT.Identity,
                scale=neg_am_01[:],
                bias=neg_modal[:, 0, 1, t : t + 1],
            )
        blend(0, 0, x_t00)
        x_t11 = transpose_x(1, 1)

        const_terms = keep.tile([P, BATCH, N_MLP + 1, NI], F32)
        nc.gpsimd.tensor_tensor(
            out=const_terms[:, :, 0:N_MLP, :],
            in0=mlp_cols[:].unsqueeze(1).to_broadcast([P, BATCH, N_MLP, NI]),
            in1=one_minus_mm[:].unsqueeze(3).to_broadcast([P, BATCH, N_MLP, NI]),
            op=ALU.mult,
        )
        nc.gpsimd.tensor_tensor(
            out=const_terms[:, :, N_MLP, :],
            in0=bias_cols[:, 0, :].unsqueeze(1).to_broadcast([P, BATCH, NI]),
            in1=bias_cols[:, 1, :].unsqueeze(1).to_broadcast([P, BATCH, NI]),
            op=ALU.add,
        )
        nc.gpsimd.tensor_scalar(
            out=a_bf[:, 0, 1],
            in0=neg_a_01[:].rearrange("p t r -> p r t"),
            scalar1=-1.0,
            scalar2=0.0,
            op0=ALU.mult,
            op1=ALU.add,
        )
        const_col = keep.tile([P, BATCH, NI], F32)
        nc.vector.tensor_reduce(
            out=const_col[:], in_=const_terms[:].rearrange("p b s i -> p b i s"), axis=AX.X, op=ALU.add
        )
        blend(1, 0, x_t10)
        blend(1, 1, x_t11)

        const_all = [psum.tile([P, D_MODEL], F32, tag="const_all%d" % b, name="const_sum%d" % b) for b in range(BATCH)]
        for b in reversed(range(BATCH)):
            for i in range(NI):
                nc.tensor.matmul(
                    out=const_all[b][:].rearrange("p (q i) -> p i q", i=NI)[:, i, :],
                    lhsT=const_col[:, b, i : i + 1].to_broadcast([P, P]),
                    rhs=ident[:],
                    is_transpose=True,
                    start=(b > 0 or i == 0),
                    stop=(b > 0),
                )
        half_a, half_b = slice(0, HALF), slice(HALF, D_MODEL)
        nc.tensor.matmul(out=const_all[0][:], lhsT=diag[:, 0, :], rhs=caches[:, 0, 0, :], start=False, stop=False)
        nc.tensor.matmul(out=const_all[0][:, half_a], lhsT=diag[:, 1, :], rhs=caches[:, 1, 0, half_a], start=False, stop=True)

        w_grouped = keep.tile([P, LAYERS, D_MODEL, PACK], BF16, align_bytes=64)
        w_codes = keep.tile([P, LAYERS, D_MODEL], U32, align_bytes=64)
        w_scales = keep.tile([P, LAYERS, D_MODEL], U8, align_bytes=64)
        def regroup(l, first_n, end_n):
            nc.scalar.copy(
                out=w_grouped[:, l, first_n:end_n].rearrange("p (g i) j -> p g j i", i=4),
                in_=w[:, l, :, first_n:end_n].rearrange("p j (g i) -> p g j i", i=4),
            )

        regroup(0, 0, D_MODEL)
        for half in range(2):
            regroup(1, half * HALF, (half + 1) * HALF)

        first = keep.tile([BATCH, D_MODEL], F32)
        nc.scalar.copy(out=first[:], in_=first_bf[:])
        nc.sync.dma_start(out=out[:, 0, :], in_=first[:])

        def quantise_w(l, first_n, end_n):
            nc.vector.quantize_mx(
                out=w_codes[:, l, first_n:end_n].bitcast(FP8X4),
                scales=w_scales[:, l, first_n:end_n],
                in_=w_grouped[:, l, first_n:end_n].rearrange("p n j -> p (n j)"),
            )

        attn = [
            [psum.tile([P, HALF], F32, tag="attn%d" % b, name="attn_a%d" % b) for b in range(BATCH)],
            [psum.tile([P, HALF], F32, tag="x_t", bufs=4, name="attn_b%d" % b) for b in range(BATCH)],
        ]

        def mx_passes(l, half):
            n = slice(half * HALF, (half + 1) * HALF)
            for b in range(BATCH):
                nc.tensor.matmul_mx(
                    out=attn[half][b][:],
                    lhsT=a_codes[:, b, l].bitcast(FP8X4),
                    lhsT_scale=a_scales[:, b, l],
                    rhs=w_codes[:, l, n].bitcast(FP8X4),
                    rhs_scale=w_scales[:, l, n],
                    start=(l == 0),
                    stop=(l == LAYERS - 1),
                )

        mlp = [keep.tile([P, D_MODEL], F32, name="mlp%d" % b) for b in range(BATCH)]

        def add_cache(b, m, earlier, n=slice(0, D_MODEL)):
            nc.vector.scalar_tensor_tensor(
                out=mlp[b][:, n],
                in0=caches[:, m, b, n],
                scalar=mm[:, b, m : m + 1],
                in1=earlier[:, n],
                op0=ALU.mult,
                op1=ALU.add,
            )

        def finish(b, half):
            n = slice(half * HALF, (half + 1) * HALF)
            result = keep.tile([P, HALF], F32, name="result%d%d" % (b, half))
            nc.vector.tensor_tensor(out=result[:], in0=attn[half][b][:], in1=mlp[b][:, n], op=ALU.add)
            nc.sync.dma_start(out=out[b, 1:POSITIONS, n], in_=result[:])

        add_cache(1, 0, const_all[1])
        quantise_a(1)
        add_cache(1, 1, mlp[1])
        quantise_a(0)
        add_cache(0, 1, const_all[0], half_b)
        quantise_w(0, 0, D_MODEL)
        mx_passes(0, 0)
        mx_passes(0, 1)
        add_cache(1, 2, mlp[1])
        quantise_w(1, 0, HALF)
        mx_passes(1, 0)
        add_cache(0, 2, const_all[0], half_a)
        add_cache(0, 2, mlp[0], half_b)
        quantise_w(1, HALF, D_MODEL)
        mx_passes(1, 1)
        finish(1, 0)
        finish(0, 0)
        finish(1, 1)
        finish(0, 1)
